import numpy as np
import ml_dtypes


def mxq(x, axis, fmt="e4m3"):
    dtype, down = {"e4m3": (ml_dtypes.float8_e4m3fn, 7), "e5m2": (ml_dtypes.float8_e5m2, 14)}[fmt]
    v = np.moveaxis(np.asarray(x, np.float32).astype(ml_dtypes.bfloat16).astype(np.float64), axis, -1)
    blocks = v.reshape(v.shape[:-1] + (-1, 32))
    amax = np.abs(blocks).max(-1, keepdims=True)
    byte = np.maximum(np.where(amax > 0, np.frexp(amax)[1] - 1 + 127, 0) - down, 1)
    scale = np.exp2(byte - 127.0)
    codes = (blocks / scale).astype(np.float32).astype(dtype).astype(np.float64)
    return np.moveaxis((codes * scale).reshape(v.shape), -1, axis)


WIDE = False


def mx_kscale(k):
    if not WIDE:
        return np.ones(k)
    levels = np.array([10, -10, 5, -5, 0])
    a = np.random.permutation(np.resize(levels, k // 512 * 4)).reshape(k // 512, 4)
    idx = np.arange(k)
    return np.exp2(a[idx // 512, idx % 128 // 32])


BF16 = ml_dtypes.bfloat16


def bf(x):
    return np.asarray(x, np.float32).astype(BF16)


def f64(x):
    return np.asarray(x).astype(np.float64)


E2M1 = np.array([0.0, 0.5, 1.0, 1.5, 2.0, 3.0, 4.0, 6.0, -0.0, -0.5, -1.0, -1.5, -2.0, -3.0, -4.0, -6.0])


def pack_weight(w, fmt):
    k, n = w.shape
    w = f64(bf(w)).reshape(k // 32, 32, n)
    amax = np.abs(w).max(1)
    if fmt == "e4m3":
        byte = np.frexp(amax)[1] - 1 + 127 - 7
    else:
        mant, ex = np.frexp(amax / 6.0)
        byte = np.where(mant > 0.5, ex, ex - 1) + 127
    byte = np.clip(np.where(amax > 0, byte, 1), 1, 254)
    scaled = (w * np.exp2(127.0 - byte)[:, None, :]).reshape(k, n).astype(np.float32)
    by_word = np.ascontiguousarray(scaled.reshape(k // 512, 128, 4, n).transpose(0, 1, 3, 2))
    if fmt == "e4m3":
        words = by_word.astype(ml_dtypes.float8_e4m3fn).view(np.uint8)
    else:
        c = by_word.astype(ml_dtypes.float4_e2m1fn).view(np.uint8) & 0xF
        words = c[..., 0::2] | (c[..., 1::2] << 4)
    return np.ascontiguousarray(words), np.ascontiguousarray(byte.astype(np.uint8).reshape(k // 512, 16, n))


def unpack_weight(words, scales, fmt):
    g, p, n, _ = words.shape
    if fmt == "e4m3":
        vals = np.ascontiguousarray(words).view(ml_dtypes.float8_e4m3fn).astype(np.float64)
    else:
        nib = np.empty((g, p, n, 4), np.uint8)
        nib[..., 0::2] = words & 0xF
        nib[..., 1::2] = words >> 4
        vals = E2M1[nib]
    vals = vals * np.repeat(np.exp2(scales.astype(np.float64) - 127.0), 8, axis=1)[..., None]
    return vals.transpose(0, 1, 3, 2).reshape(g * 512, n)

def pack4(w):
    words, scales = pack_weight(w, "e2m1")
    return words.reshape(words.shape[0], 128, -1), scales


def unpack4(words, scales):
    return unpack_weight(words.reshape(words.shape[0], 128, -1, 2), scales, "e2m1")


BATCH, IN_F, OUT_F, RANK, N_ADAPTERS = 1024, 2048, 2048, 128, 8
SEG = BATCH // N_ADAPTERS
LORA_GAIN = 2.0


def setup_inputs():
    s = mx_kscale(IN_F)
    x = bf(np.random.standard_normal((BATCH, IN_F)) * s)
    h_lora = bf(np.random.standard_normal((N_ADAPTERS, SEG, RANK)))
    lora_B = bf(np.random.standard_normal((N_ADAPTERS, RANK, OUT_F)) * 0.5 / np.sqrt(RANK))
    words, scales = pack4(np.random.standard_normal((IN_F, OUT_F)) / np.sqrt(IN_F) / s[:, None])
    return {"x": x,
            "h_lora": h_lora,
            "lora_B": lora_B,
            "M_words": words,
            "M_scales": scales}


def reference(x, h_lora, lora_B, M_words, M_scales):
    y = (f64(h_lora) @ f64(lora_B)) * LORA_GAIN
    y = y.reshape(BATCH, OUT_F)
    return y + (mxq(f64(x), 1, "e4m3") @ unpack4(M_words, M_scales))

@@ -1,0 +1,171 @@
+from contextlib import ExitStack
+
+import concourse.mybir as mybir
+from concourse.masks import make_identity
+
+BF16 = mybir.dt.bfloat16
+F32 = mybir.dt.float32
+I32 = mybir.dt.int32
+U32 = mybir.dt.uint32
+U8 = mybir.dt.uint8
+FP8X4 = mybir.dt.float8_e4m3fn_x4
+FP4X4 = mybir.dt.float4_e2m1fn_x4
+
+P = 128
+ROWS, IN_F, OUT_F = 1024, 2048, 2048
+SEGMENTS = ROWS // P
+K_PASS = 4 * P
+PASSES = IN_F // K_PASS
+WORDS_PASS = K_PASS // 2
+BANK = 512
+BANKS_HALF = 2
+HALF = BANK * BANKS_HALF
+HALVES = OUT_F // HALF
+LORA_GAIN = 2.0
+
+FLOPS = 2 * ROWS * IN_F * OUT_F + 2 * ROWS * P * OUT_F
+
+
+def tile_lorasequential_pa_kernel(tc, x, h_lora, lora_B, M_words, M_scales, out):
+    nc = tc.nc
+    with ExitStack() as stack:
+        resident = stack.enter_context(tc.tile_pool(name="resident", bufs=1))
+        operand = stack.enter_context(tc.tile_pool(name="operand", bufs=2))
+        turned_pool = stack.enter_context(tc.psum_pool(name="turned_pool", bufs=2))
+        lora_pool = stack.enter_context(tc.psum_pool(name="lora_pool", bufs=2))
+        base_pool = stack.enter_context(tc.psum_pool(name="base_pool", bufs=2 * BANKS_HALF))
+
+        x_sb = [resident.tile([P, IN_F], BF16, name="x_sb%d" % s) for s in range(SEGMENTS)]
+        b_sb = [resident.tile([P, OUT_F], BF16, name="b_sb%d" % s) for s in range(SEGMENTS)]
+        out_sb = [resident.tile([P, OUT_F], F32, name="out_sb%d" % s) for s in range(SEGMENTS)]
+        h_sb = resident.tile([P, SEGMENTS, P], BF16)
+        hT_sb = resident.tile([P, ROWS], BF16)
+        m_words = resident.tile([P, PASSES, 2 * OUT_F], U8, align_bytes=64)
+        m_scales = resident.tile([P, PASSES, OUT_F], U8, align_bytes=64)
+        ident_f32 = resident.tile([P, P], F32)
+        ident_bf16 = resident.tile([P, P], BF16)
+
+        make_identity(nc, ident_f32[:])
+        make_identity(nc, ident_bf16[:])
+
+        for pair in range(PASSES // 2):
+            nc.vector.memset(
+                m_scales[:, 2 * pair : 2 * pair + 2, :].rearrange("p g n -> p (g n)").bitcast(I32), 0
+            )
+
+        def load_x(s):
+            nc.sync.dma_start(out=x_sb[s][:], in_=x[P * s : P * (s + 1), :])
+
+        def load_lora_b(s):
+            nc.sync.dma_start(out=b_sb[s][:], in_=lora_B[s])
+
+        def load_h():
+            nc.sync.dma_start(
+                out=h_sb[:], in_=h_lora.rearrange("s b r -> (s b) r").rearrange("(p j) r -> p j r", j=SEGMENTS)
+            )
+
+        def load_m_scales():
+            for pair in range(PASSES // 2):
+                passes = slice(2 * pair, 2 * pair + 2)
+                for q in range(8):
+                    first = 32 * (q // 4) + q % 4
+                    nc.sync.dma_start(
+                        out=m_scales[first:P:64, passes, :].bitcast(I32),
+                        in_=M_scales[passes, q:16:8, :].rearrange("g q n -> q g n").bitcast(I32),
+                    )
+
+        def load_m_words(half):
+            byte_cols = slice(2 * HALF * half, 2 * HALF * (half + 1))
+            for g in range(PASSES):
+                nc.sync.dma_start(
+                    out=m_words[:, g, byte_cols].bitcast(I32), in_=M_words[g, :, byte_cols].bitcast(I32)
+                )
+
+        load_x(0)
+        load_h()
+        load_lora_b(0)
+        load_m_scales()
+        load_m_words(0)
+        load_x(1)
+        load_m_words(1)
+        for s in range(1, SEGMENTS):
+            load_lora_b(s)
+            if s + 1 < SEGMENTS:
+                load_x(s + 1)
+
+        def turn_x(s):
+            words = x_sb[s][:].bitcast(F32)
+            grouped = operand.tile([P, IN_F], BF16, align_bytes=64)
+            grouped_words = grouped[:].bitcast(F32).rearrange("p (g r u) -> p g r u", r=P, u=2)
+            for pair in range(PASSES // 2):
+                turned = turned_pool.tile([P, 4, P], F32, tag="turned")
+                for j in range(4):
+                    g, u = 2 * pair + j // 2, j % 2
+                    nc.tensor.transpose(
+                        turned[:, j, :], words[:, WORDS_PASS * g + u : WORDS_PASS * (g + 1) : 2], ident_f32[:]
+                    )
+                nc.scalar.copy(
+                    out=grouped_words[:, 2 * pair : 2 * pair + 2, :, :],
+                    in_=turned[:].rearrange("p (g u) r -> p g r u", u=2),
+                )
+            return grouped
+
+        def quantise_x(grouped):
+            codes = operand.tile([P, PASSES * P], U32, align_bytes=64)
+            scales = operand.tile([P, PASSES * P], U8, align_bytes=64)
+            nc.vector.quantize_mx(out=codes[:].bitcast(FP8X4), scales=scales[:], in_=grouped[:])
+            return codes, scales
+
+        def turn_h():
+            hT_ps = turned_pool.tile([P, SEGMENTS, P], BF16, tag="turned")
+            for j in range(SEGMENTS):
+                nc.tensor.transpose(hT_ps[:, j, :], h_sb[:, j, :], ident_bf16[:])
+            nc.vector.tensor_copy(
+                out=hT_sb[:].rearrange("r (p j) -> r p j", j=SEGMENTS), in_=hT_ps[:].rearrange("r j p -> r p j")
+            )
+
+        def lora_block(s, n):
+            cols = slice(BANK * n, BANK * (n + 1))
+            low_rank = lora_pool.tile([P, BANK], F32)
+            nc.tensor.matmul(
+                out=low_rank[:], lhsT=hT_sb[:, P * s : P * (s + 1)], rhs=b_sb[s][:, cols], start=True, stop=True
+            )
+            nc.scalar.mul(out=out_sb[s][:, cols], in_=low_rank[:], mul=LORA_GAIN)
+
+        def base_half(s, half, codes, scales):
+            blocks = range(BANKS_HALF * half, BANKS_HALF * (half + 1))
+            sums = [base_pool.tile([P, BANK], F32, name="base_sum", tag="base_sum") for n in blocks]
+            for g in range(PASSES):
+                rows = slice(P * g, P * (g + 1))
+                for base_sum, n in zip(sums, blocks):
+                    nc.tensor.matmul_mx(
+                        out=base_sum[:],
+                        lhsT=codes[:, rows].bitcast(FP8X4),
+                        lhsT_scale=scales[:, rows],
+                        rhs=m_words[:, g, 2 * BANK * n : 2 * BANK * (n + 1)].bitcast(FP4X4),
+                        rhs_scale=m_scales[:, g, BANK * n : BANK * (n + 1)],
+                        start=(g == 0),
+                        stop=(g == PASSES - 1),
+                    )
+            for base_sum, n in zip(sums, blocks):
+                cols = slice(BANK * n, BANK * (n + 1))
+                nc.vector.tensor_tensor(
+                    out=out_sb[s][:, cols], in0=base_sum[:], in1=out_sb[s][:, cols], op=mybir.AluOpType.add
+                )
+                nc.sync.dma_start(out=out[P * s : P * (s + 1), cols], in_=out_sb[s][:, cols])
+
+        grouped = turn_x(0)
+        turn_h()
+        codes, scales = quantise_x(grouped)
+        for s in range(SEGMENTS):
+            lora_block(s, 0)
+            lora_block(s, 1)
+            base_half(s, 0, codes, scales)
+            if s + 1 < SEGMENTS:
+                grouped = turn_x(s + 1)
+            lora_block(s, 2)
+            lora_block(s, 3)
+            if s + 1 < SEGMENTS:
+                next_codes, next_scales = quantise_x(grouped)
+            base_half(s, 1, codes, scales)
+            codes, scales = next_codes, next_scales

@@ -16,7 +16,6 @@ ROWS, IN_F, OUT_F = 1024, 2048, 2048
 SEGMENTS = ROWS // P
 K_PASS = 4 * P
 PASSES = IN_F // K_PASS
-WORDS_PASS = K_PASS // 2
 BANK = 512
 BANKS_HALF = 2
 HALF = BANK * BANKS_HALF
@@ -68,9 +67,9 @@ def tile_lorasequential_pa_kernel(tc, x, h_lora, lora_B, M_words, M_scales, out)
             for pair in range(PASSES // 2):
                 passes = slice(2 * pair, 2 * pair + 2)
                 for q in range(8):
-                    first = 32 * (q // 4) + q % 4
+                    first_partition = 32 * (q // 4) + q % 4
                     nc.sync.dma_start(
-                        out=m_scales[first:P:64, passes, :].bitcast(I32),
+                        out=m_scales[first_partition:P:64, passes, :].bitcast(I32),
                         in_=M_scales[passes, q:16:8, :].rearrange("g q n -> q g n").bitcast(I32),
                     )
 
@@ -93,17 +92,22 @@ def tile_lorasequential_pa_kernel(tc, x, h_lora, lora_B, M_words, M_scales, out)
             if s + 1 < SEGMENTS:
                 load_x(s + 1)
 
-        def turn_x(s):
-            words = x_sb[s][:].bitcast(F32)
+        def sort_x(s):
+            sorted_words = operand.tile([P, IN_F // 2], F32)
+            nc.vector.tensor_copy(
+                out=sorted_words[:].rearrange("r (g u p) -> r g u p", u=2, p=P),
+                in_=x_sb[s][:].bitcast(F32).rearrange("r (g p u) -> r g u p", u=2, p=P),
+            )
+            return sorted_words
+
+        def turn_x(sorted_words):
             grouped = operand.tile([P, IN_F], BF16, align_bytes=64)
             grouped_words = grouped[:].bitcast(F32).rearrange("p (g r u) -> p g r u", r=P, u=2)
             for pair in range(PASSES // 2):
                 turned = turned_pool.tile([P, 4, P], F32, tag="turned")
                 for j in range(4):
-                    g, u = 2 * pair + j // 2, j % 2
-                    nc.tensor.transpose(
-                        turned[:, j, :], words[:, WORDS_PASS * g + u : WORDS_PASS * (g + 1) : 2], ident_f32[:]
-                    )
+                    first_word = P * (4 * pair + j)
+                    nc.tensor.transpose(turned[:, j, :], sorted_words[:, first_word : first_word + P], ident_f32[:])
                 nc.scalar.copy(
                     out=grouped_words[:, 2 * pair : 2 * pair + 2, :, :],
                     in_=turned[:].rearrange("p (g u) r -> p g r u", u=2),
@@ -154,15 +158,17 @@ def tile_lorasequential_pa_kernel(tc, x, h_lora, lora_B, M_words, M_scales, out)
                 )
                 nc.sync.dma_start(out=out[P * s : P * (s + 1), cols], in_=out_sb[s][:, cols])
 
-        grouped = turn_x(0)
+        grouped = turn_x(sort_x(0))
         turn_h()
         codes, scales = quantise_x(grouped)
         for s in range(SEGMENTS):
+            if s + 1 < SEGMENTS:
+                sorted_words = sort_x(s + 1)
             lora_block(s, 0)
             lora_block(s, 1)
             base_half(s, 0, codes, scales)
             if s + 1 < SEGMENTS:
-                grouped = turn_x(s + 1)
+                grouped = turn_x(sorted_words)
             lora_block(s, 2)
             lora_block(s, 3)
             if s + 1 < SEGMENTS:

@@ -14,12 +14,12 @@ FP4X4 = mybir.dt.float4_e2m1fn_x4
 P = 128
 ROWS, IN_F, OUT_F = 1024, 2048, 2048
 SEGMENTS = ROWS // P
+PAIRS = SEGMENTS // 2
 K_PASS = 4 * P
 PASSES = IN_F // K_PASS
 BANK = 512
-BANKS_HALF = 2
-HALF = BANK * BANKS_HALF
-HALVES = OUT_F // HALF
+BLOCKS = OUT_F // BANK
+HALF = OUT_F // 2
 LORA_GAIN = 2.0
 
 FLOPS = 2 * ROWS * IN_F * OUT_F + 2 * ROWS * P * OUT_F
@@ -29,10 +29,11 @@ def tile_lorasequential_pa_kernel(tc, x, h_lora, lora_B, M_words, M_scales, out)
     nc = tc.nc
     with ExitStack() as stack:
         resident = stack.enter_context(tc.tile_pool(name="resident", bufs=1))
-        operand = stack.enter_context(tc.tile_pool(name="operand", bufs=2))
+        operand = stack.enter_context(tc.tile_pool(name="operand", bufs=4))
         turned_pool = stack.enter_context(tc.psum_pool(name="turned_pool", bufs=2))
         lora_pool = stack.enter_context(tc.psum_pool(name="lora_pool", bufs=2))
-        base_pool = stack.enter_context(tc.psum_pool(name="base_pool", bufs=2 * BANKS_HALF))
+        base_pool = stack.enter_context(tc.psum_pool(name="base_pool", bufs=4))
+        stack.enter_context(tc.manual_schedule())
 
         x_sb = [resident.tile([P, IN_F], BF16, name="x_sb%d" % s) for s in range(SEGMENTS)]
         b_sb = [resident.tile([P, OUT_F], BF16, name="b_sb%d" % s) for s in range(SEGMENTS)]
@@ -47,9 +48,13 @@ def tile_lorasequential_pa_kernel(tc, x, h_lora, lora_B, M_words, M_scales, out)
         make_identity(nc, ident_f32[:])
         make_identity(nc, ident_bf16[:])
 
-        for pair in range(PASSES // 2):
+        warm = resident.tile([P, 1], F32)
+        nc.vector.memset(warm[:], 0.0)
+        nc.scalar.mul(out=warm[:], in_=warm[:], mul=LORA_GAIN)
+
+        for two in range(PASSES // 2):
             nc.vector.memset(
-                m_scales[:, 2 * pair : 2 * pair + 2, :].rearrange("p g n -> p (g n)").bitcast(I32), 0
+                m_scales[:, 2 * two : 2 * two + 2, :].rearrange("p g n -> p (g n)").bitcast(I32), 0
             )
 
         def load_x(s):
@@ -64,14 +69,12 @@ def tile_lorasequential_pa_kernel(tc, x, h_lora, lora_B, M_words, M_scales, out)
             )
 
         def load_m_scales():
-            for pair in range(PASSES // 2):
-                passes = slice(2 * pair, 2 * pair + 2)
-                for q in range(8):
-                    first_partition = 32 * (q // 4) + q % 4
-                    nc.sync.dma_start(
-                        out=m_scales[first_partition:P:64, passes, :].bitcast(I32),
-                        in_=M_scales[passes, q:16:8, :].rearrange("g q n -> q g n").bitcast(I32),
-                    )
+            for q in range(8):
+                first_partition = 32 * (q // 4) + q % 4
+                nc.sync.dma_start(
+                    out=m_scales[first_partition:P:64, :, :].bitcast(I32),
+                    in_=M_scales[:, q:16:8, :].rearrange("g q n -> q g n").bitcast(I32),
+                )
 
         def load_m_words(half):
             byte_cols = slice(2 * HALF * half, 2 * HALF * (half + 1))
@@ -81,16 +84,21 @@ def tile_lorasequential_pa_kernel(tc, x, h_lora, lora_B, M_words, M_scales, out)
                 )
 
         load_x(0)
-        load_h()
-        load_lora_b(0)
+        load_x(1)
         load_m_scales()
         load_m_words(0)
-        load_x(1)
+        load_h()
+        load_lora_b(0)
+        load_lora_b(1)
+        load_x(2)
+        load_x(3)
         load_m_words(1)
-        for s in range(1, SEGMENTS):
-            load_lora_b(s)
-            if s + 1 < SEGMENTS:
-                load_x(s + 1)
+        for pair in range(1, PAIRS):
+            load_lora_b(2 * pair)
+            load_lora_b(2 * pair + 1)
+            if pair + 1 < PAIRS:
+                load_x(2 * pair + 2)
+                load_x(2 * pair + 3)
 
         def sort_x(s):
             sorted_words = operand.tile([P, IN_F // 2], F32)
@@ -103,13 +111,13 @@ def tile_lorasequential_pa_kernel(tc, x, h_lora, lora_B, M_words, M_scales, out)
         def turn_x(sorted_words):
             grouped = operand.tile([P, IN_F], BF16, align_bytes=64)
             grouped_words = grouped[:].bitcast(F32).rearrange("p (g r u) -> p g r u", r=P, u=2)
-            for pair in range(PASSES // 2):
+            for two in range(PASSES // 2):
                 turned = turned_pool.tile([P, 4, P], F32, tag="turned")
                 for j in range(4):
-                    first_word = P * (4 * pair + j)
+                    first_word = P * (4 * two + j)
                     nc.tensor.transpose(turned[:, j, :], sorted_words[:, first_word : first_word + P], ident_f32[:])
                 nc.scalar.copy(
-                    out=grouped_words[:, 2 * pair : 2 * pair + 2, :, :],
+                    out=grouped_words[:, 2 * two : 2 * two + 2, :, :],
                     in_=turned[:].rearrange("p (g u) r -> p g r u", u=2),
                 )
             return grouped
@@ -128,20 +136,21 @@ def tile_lorasequential_pa_kernel(tc, x, h_lora, lora_B, M_words, M_scales, out)
                 out=hT_sb[:].rearrange("r (p j) -> r p j", j=SEGMENTS), in_=hT_ps[:].rearrange("r j p -> r p j")
             )
 
-        def lora_block(s, n):
+        def lora_products(pair, n):
             cols = slice(BANK * n, BANK * (n + 1))
-            low_rank = lora_pool.tile([P, BANK], F32)
-            nc.tensor.matmul(
-                out=low_rank[:], lhsT=hT_sb[:, P * s : P * (s + 1)], rhs=b_sb[s][:, cols], start=True, stop=True
-            )
-            nc.scalar.mul(out=out_sb[s][:, cols], in_=low_rank[:], mul=LORA_GAIN)
+            for s in (2 * pair, 2 * pair + 1):
+                low_rank = lora_pool.tile([P, BANK], F32)
+                nc.tensor.matmul(
+                    out=low_rank[:], lhsT=hT_sb[:, P * s : P * (s + 1)], rhs=b_sb[s][:, cols], start=True, stop=True
+                )
+                nc.scalar.mul(out=out_sb[s][:, cols], in_=low_rank[:], mul=LORA_GAIN)
 
-        def base_half(s, half, codes, scales):
-            blocks = range(BANKS_HALF * half, BANKS_HALF * (half + 1))
-            sums = [base_pool.tile([P, BANK], F32, name="base_sum", tag="base_sum") for n in blocks]
-            for g in range(PASSES):
-                rows = slice(P * g, P * (g + 1))
-                for base_sum, n in zip(sums, blocks):
+        def base_passes(n, quantised):
+            sums = []
+            for codes, scales in quantised:
+                base_sum = base_pool.tile([P, BANK], F32)
+                for g in range(PASSES):
+                    rows = slice(P * g, P * (g + 1))
                     nc.tensor.matmul_mx(
                         out=base_sum[:],
                         lhsT=codes[:, rows].bitcast(FP8X4),
@@ -151,27 +160,38 @@ def tile_lorasequential_pa_kernel(tc, x, h_lora, lora_B, M_words, M_scales, out)
                         start=(g == 0),
                         stop=(g == PASSES - 1),
                     )
-            for base_sum, n in zip(sums, blocks):
-                cols = slice(BANK * n, BANK * (n + 1))
+                sums.append(base_sum)
+            return sums
+
+        def add_and_store(pair, n, sums):
+            cols = slice(BANK * n, BANK * (n + 1))
+            for base_sum, s in zip(sums, (2 * pair, 2 * pair + 1)):
                 nc.vector.tensor_tensor(
                     out=out_sb[s][:, cols], in0=base_sum[:], in1=out_sb[s][:, cols], op=mybir.AluOpType.add
                 )
                 nc.sync.dma_start(out=out[P * s : P * (s + 1), cols], in_=out_sb[s][:, cols])
 
-        grouped = turn_x(sort_x(0))
-        turn_h()
-        codes, scales = quantise_x(grouped)
-        for s in range(SEGMENTS):
-            if s + 1 < SEGMENTS:
-                sorted_words = sort_x(s + 1)
-            lora_block(s, 0)
-            lora_block(s, 1)
-            base_half(s, 0, codes, scales)
-            if s + 1 < SEGMENTS:
-                grouped = turn_x(sorted_words)
-            lora_block(s, 2)
-            lora_block(s, 3)
-            if s + 1 < SEGMENTS:
-                next_codes, next_scales = quantise_x(grouped)
-            base_half(s, 1, codes, scales)
-            codes, scales = next_codes, next_scales
+        grouped = [turn_x(sort_x(s)) for s in (0, 1)]
+        quantised = [quantise_x(grouped_x) for grouped_x in grouped]
+        for pair in range(PAIRS):
+            more = pair + 1 < PAIRS
+            if pair == 0:
+                early_sums = [base_passes(0, quantised)]
+                turn_h()
+                early_sums.append(base_passes(1, quantised))
+            if more:
+                sorted_next = [sort_x(s) for s in (2 * pair + 2, 2 * pair + 3)]
+            for n in (0, 1):
+                lora_products(pair, n)
+                add_and_store(pair, n, early_sums[n] if pair == 0 else base_passes(n, quantised))
+            if more:
+                grouped = [turn_x(sorted_next[0])]
+            lora_products(pair, 2)
+            add_and_store(pair, 2, base_passes(2, quantised))
+            if more:
+                grouped.append(turn_x(sorted_next[1]))
+            lora_products(pair, 3)
+            last_sums = base_passes(3, quantised)
+            if more:
+                quantised = [quantise_x(grouped_x) for grouped_x in grouped]
+            add_and_store(pair, 3, last_sums)

@@ -10,6 +10,8 @@ U32 = mybir.dt.uint32
 U8 = mybir.dt.uint8
 FP8X4 = mybir.dt.float8_e4m3fn_x4
 FP4X4 = mybir.dt.float4_e2m1fn_x4
+ADD = mybir.AluOpType.add
+MULT = mybir.AluOpType.mult
 
 P = 128
 ROWS, IN_F, OUT_F = 1024, 2048, 2048
@@ -19,8 +21,10 @@ K_PASS = 4 * P
 PASSES = IN_F // K_PASS
 BANK = 512
 BLOCKS = OUT_F // BANK
-HALF = OUT_F // 2
 LORA_GAIN = 2.0
+
+TAIL_SPLIT = False
+DUMMIES = 0
 
 FLOPS = 2 * ROWS * IN_F * OUT_F + 2 * ROWS * P * OUT_F
 
@@ -30,9 +34,9 @@ def tile_lorasequential_pa_kernel(tc, x, h_lora, lora_B, M_words, M_scales, out)
     with ExitStack() as stack:
         resident = stack.enter_context(tc.tile_pool(name="resident", bufs=1))
         operand = stack.enter_context(tc.tile_pool(name="operand", bufs=4))
-        turned_pool = stack.enter_context(tc.psum_pool(name="turned_pool", bufs=2))
+        turned_pool = stack.enter_context(tc.psum_pool(name="turned_pool", bufs=3))
         lora_pool = stack.enter_context(tc.psum_pool(name="lora_pool", bufs=2))
-        base_pool = stack.enter_context(tc.psum_pool(name="base_pool", bufs=4))
+        base_pool = stack.enter_context(tc.psum_pool(name="base_pool", bufs=3))
         stack.enter_context(tc.manual_schedule())
 
         x_sb = [resident.tile([P, IN_F], BF16, name="x_sb%d" % s) for s in range(SEGMENTS)]
@@ -40,8 +44,8 @@ def tile_lorasequential_pa_kernel(tc, x, h_lora, lora_B, M_words, M_scales, out)
         out_sb = [resident.tile([P, OUT_F], F32, name="out_sb%d" % s) for s in range(SEGMENTS)]
         h_sb = resident.tile([P, SEGMENTS, P], BF16)
         hT_sb = resident.tile([P, ROWS], BF16)
-        m_words = resident.tile([P, PASSES, 2 * OUT_F], U8, align_bytes=64)
-        m_scales = resident.tile([P, PASSES, OUT_F], U8, align_bytes=64)
+        m_words = resident.tile([P, BLOCKS, PASSES, 2 * BANK], U8, align_bytes=64)
+        m_scales = resident.tile([P, BLOCKS, PASSES, BANK], U8, align_bytes=64)
         ident_f32 = resident.tile([P, P], F32)
         ident_bf16 = resident.tile([P, P], BF16)
 
@@ -52,13 +56,14 @@ def tile_lorasequential_pa_kernel(tc, x, h_lora, lora_B, M_words, M_scales, out)
         nc.vector.memset(warm[:], 0.0)
         nc.scalar.mul(out=warm[:], in_=warm[:], mul=LORA_GAIN)
 
-        for two in range(PASSES // 2):
-            nc.vector.memset(
-                m_scales[:, 2 * two : 2 * two + 2, :].rearrange("p g n -> p (g n)").bitcast(I32), 0
-            )
+        for n in range(BLOCKS):
+            nc.vector.memset(m_scales[:, n, :, :].rearrange("p g c -> p (g c)").bitcast(I32), 0)
 
-        def load_x(s):
-            nc.sync.dma_start(out=x_sb[s][:], in_=x[P * s : P * (s + 1), :])
+        def load_x(s, pieces):
+            width = IN_F // pieces
+            for piece in range(pieces):
+                cols = slice(width * piece, width * (piece + 1))
+                nc.sync.dma_start(out=x_sb[s][:, cols], in_=x[P * s : P * (s + 1), cols])
 
         def load_lora_b(s):
             nc.sync.dma_start(out=b_sb[s][:], in_=lora_B[s])
@@ -68,65 +73,80 @@ def tile_lorasequential_pa_kernel(tc, x, h_lora, lora_B, M_words, M_scales, out)
                 out=h_sb[:], in_=h_lora.rearrange("s b r -> (s b) r").rearrange("(p j) r -> p j r", j=SEGMENTS)
             )
 
-        def load_m_scales():
-            for q in range(8):
-                first_partition = 32 * (q // 4) + q % 4
+        def load_m_block(n, pieces):
+            cols = slice(BANK * n, BANK * (n + 1))
+            for r in range(4):
                 nc.sync.dma_start(
-                    out=m_scales[first_partition:P:64, :, :].bitcast(I32),
-                    in_=M_scales[:, q:16:8, :].rearrange("g q n -> q g n").bitcast(I32),
+                    out=m_scales[r:P:32, n, :, :].bitcast(I32),
+                    in_=M_scales[:, r:16:4, cols].rearrange("g q c -> q g c").bitcast(I32),
+                )
+            byte_cols = slice(2 * BANK * n, 2 * BANK * (n + 1))
+            count = PASSES // pieces
+            for piece in range(pieces):
+                some = slice(count * piece, count * (piece + 1))
+                nc.sync.dma_start(
+                    out=m_words[:, n, some, :].bitcast(I32),
+                    in_=M_words[some, :, byte_cols].rearrange("g p c -> p g c").bitcast(I32),
                 )
 
-        def load_m_words(half):
-            byte_cols = slice(2 * HALF * half, 2 * HALF * (half + 1))
-            for g in range(PASSES):
-                nc.sync.dma_start(
-                    out=m_words[:, g, byte_cols].bitcast(I32), in_=M_words[g, :, byte_cols].bitcast(I32)
-                )
-
-        load_x(0)
-        load_x(1)
-        load_m_scales()
-        load_m_words(0)
+        load_x(0, 2)
+        load_x(1, 2)
+        load_m_block(0, 2)
+        load_m_block(1, 1)
         load_h()
         load_lora_b(0)
         load_lora_b(1)
-        load_x(2)
-        load_x(3)
-        load_m_words(1)
+        load_m_block(2, 1)
+        load_x(2, 1)
+        load_x(3, 1)
+        load_m_block(3, 1)
         for pair in range(1, PAIRS):
             load_lora_b(2 * pair)
             load_lora_b(2 * pair + 1)
             if pair + 1 < PAIRS:
-                load_x(2 * pair + 2)
-                load_x(2 * pair + 3)
+                load_x(2 * pair + 2, 1)
+                load_x(2 * pair + 3, 1)
 
         def sort_x(s):
-            sorted_words = operand.tile([P, IN_F // 2], F32)
+            sorted_words = operand.tile([P, IN_F // 2], F32, tag="sorted_words")
             nc.vector.tensor_copy(
                 out=sorted_words[:].rearrange("r (g u p) -> r g u p", u=2, p=P),
                 in_=x_sb[s][:].bitcast(F32).rearrange("r (g p u) -> r g u p", u=2, p=P),
             )
             return sorted_words
 
-        def turn_x(sorted_words):
-            grouped = operand.tile([P, IN_F], BF16, align_bytes=64)
+        def turn_two_passes(words, is_sorted, two, grouped):
+            turned = turned_pool.tile([P, 4, P], F32, tag="turned")
+            for j in range(4):
+                if is_sorted:
+                    source = words[:, P * (4 * two + j) : P * (4 * two + j + 1)]
+                else:
+                    g, u = 2 * two + j // 2, j % 2
+                    source = words[:, 2 * P * g + u : 2 * P * (g + 1) : 2]
+                nc.tensor.transpose(turned[:, j, :], source, ident_f32[:])
             grouped_words = grouped[:].bitcast(F32).rearrange("p (g r u) -> p g r u", r=P, u=2)
-            for two in range(PASSES // 2):
-                turned = turned_pool.tile([P, 4, P], F32, tag="turned")
-                for j in range(4):
-                    first_word = P * (4 * two + j)
-                    nc.tensor.transpose(turned[:, j, :], sorted_words[:, first_word : first_word + P], ident_f32[:])
-                nc.scalar.copy(
-                    out=grouped_words[:, 2 * two : 2 * two + 2, :, :],
-                    in_=turned[:].rearrange("p (g u) r -> p g r u", u=2),
-                )
+            nc.scalar.copy(
+                out=grouped_words[:, 2 * two : 2 * two + 2, :, :],
+                in_=turned[:].rearrange("p (g u) r -> p g r u", u=2),
+            )
+
+        def new_grouped():
+            grouped = operand.tile([P, IN_F], BF16, align_bytes=64, tag="grouped")
             return grouped
 
-        def quantise_x(grouped):
-            codes = operand.tile([P, PASSES * P], U32, align_bytes=64)
-            scales = operand.tile([P, PASSES * P], U8, align_bytes=64)
-            nc.vector.quantize_mx(out=codes[:].bitcast(FP8X4), scales=scales[:], in_=grouped[:])
+        def new_quantised():
+            codes = operand.tile([P, PASSES * P], U32, align_bytes=64, tag="codes")
+            scales = operand.tile([P, PASSES * P], U8, align_bytes=64, tag="scales")
             return codes, scales
+
+        def quantise(grouped, quantised, first_pass, passes):
+            codes, scales = quantised
+            cols = slice(P * first_pass, P * (first_pass + passes))
+            nc.vector.quantize_mx(
+                out=codes[:, cols].bitcast(FP8X4),
+                scales=scales[:, cols],
+                in_=grouped[:, 4 * P * first_pass : 4 * P * (first_pass + passes)],
+            )
 
         def turn_h():
             hT_ps = turned_pool.tile([P, SEGMENTS, P], BF16, tag="turned")
@@ -136,62 +156,124 @@ def tile_lorasequential_pa_kernel(tc, x, h_lora, lora_B, M_words, M_scales, out)
                 out=hT_sb[:].rearrange("r (p j) -> r p j", j=SEGMENTS), in_=hT_ps[:].rearrange("r j p -> r p j")
             )
 
-        def lora_products(pair, n):
-            cols = slice(BANK * n, BANK * (n + 1))
-            for s in (2 * pair, 2 * pair + 1):
-                low_rank = lora_pool.tile([P, BANK], F32)
-                nc.tensor.matmul(
-                    out=low_rank[:], lhsT=hT_sb[:, P * s : P * (s + 1)], rhs=b_sb[s][:, cols], start=True, stop=True
+        def lora_product(s, n):
+            low_rank = lora_pool.tile([P, BANK], F32, tag="low_rank")
+            nc.tensor.matmul(
+                out=low_rank[:],
+                lhsT=hT_sb[:, P * s : P * (s + 1)],
+                rhs=b_sb[s][:, BANK * n : BANK * (n + 1)],
+                start=True,
+                stop=True,
+            )
+            return low_rank
+
+        def lora_first(s, n):
+            nc.scalar.mul(out=out_sb[s][:, BANK * n : BANK * (n + 1)], in_=lora_product(s, n)[:], mul=LORA_GAIN)
+
+        def group(n, quantised, first_col, width):
+            codes, scales = quantised
+            base_sum = base_pool.tile([P, BANK], F32, tag="base_sum")
+            for g in range(PASSES):
+                rows = slice(P * g, P * (g + 1))
+                nc.tensor.matmul_mx(
+                    out=base_sum[:, 0:width],
+                    lhsT=codes[:, rows].bitcast(FP8X4),
+                    lhsT_scale=scales[:, rows],
+                    rhs=m_words[:, n, g, 2 * first_col : 2 * (first_col + width)].bitcast(FP4X4),
+                    rhs_scale=m_scales[:, n, g, first_col : first_col + width],
+                    start=(g == 0),
+                    stop=(g == PASSES - 1),
                 )
-                nc.scalar.mul(out=out_sb[s][:, cols], in_=low_rank[:], mul=LORA_GAIN)
+            return base_sum
 
-        def base_passes(n, quantised):
-            sums = []
-            for codes, scales in quantised:
-                base_sum = base_pool.tile([P, BANK], F32)
-                for g in range(PASSES):
-                    rows = slice(P * g, P * (g + 1))
-                    nc.tensor.matmul_mx(
-                        out=base_sum[:],
-                        lhsT=codes[:, rows].bitcast(FP8X4),
-                        lhsT_scale=scales[:, rows],
-                        rhs=m_words[:, g, 2 * BANK * n : 2 * BANK * (n + 1)].bitcast(FP4X4),
-                        rhs_scale=m_scales[:, g, BANK * n : BANK * (n + 1)],
-                        start=(g == 0),
-                        stop=(g == PASSES - 1),
-                    )
-                sums.append(base_sum)
-            return sums
+        def store(s, cols):
+            nc.sync.dma_start(out=out[P * s : P * (s + 1), cols], in_=out_sb[s][:, cols])
 
-        def add_and_store(pair, n, sums):
-            cols = slice(BANK * n, BANK * (n + 1))
-            for base_sum, s in zip(sums, (2 * pair, 2 * pair + 1)):
-                nc.vector.tensor_tensor(
-                    out=out_sb[s][:, cols], in0=base_sum[:], in1=out_sb[s][:, cols], op=mybir.AluOpType.add
-                )
-                nc.sync.dma_start(out=out[P * s : P * (s + 1), cols], in_=out_sb[s][:, cols])
+        def add_and_store(s, n, base_sum, first_col, width):
+            cols = slice(BANK * n + first_col, BANK * n + first_col + width)
+            nc.vector.tensor_tensor(out=out_sb[s][:, cols], in0=base_sum[:, 0:width], in1=out_sb[s][:, cols], op=ADD)
+            store(s, cols)
 
-        grouped = [turn_x(sort_x(s)) for s in (0, 1)]
-        quantised = [quantise_x(grouped_x) for grouped_x in grouped]
+        def block(s, n, quantised):
+            add_and_store(s, n, group(n, quantised, 0, BANK), 0, BANK)
+
+        if DUMMIES:
+            zeros = resident.tile([P, BANK], BF16)
+            nc.gpsimd.memset(zeros[:], 0.0)
+
+        def dummies(count):
+            for i in range(count):
+                idle = lora_pool.tile([P, BANK], F32, tag="low_rank")
+                nc.tensor.matmul(out=idle[:], lhsT=zeros[:, 0:P], rhs=zeros[:], start=True, stop=True)
+
+        if DUMMIES:
+            dummies(DUMMIES)
+
+        quantised = []
+        for s in (0, 1):
+            grouped = new_grouped()
+            fresh = new_quantised()
+            for two in range(PASSES // 2):
+                turn_two_passes(x_sb[s][:].bitcast(F32), False, two, grouped)
+                quantise(grouped, fresh, 2 * two, 2)
+            quantised.append(fresh)
+
         for pair in range(PAIRS):
+            a, b = 2 * pair, 2 * pair + 1
             more = pair + 1 < PAIRS
             if pair == 0:
-                early_sums = [base_passes(0, quantised)]
+                for n in (0, 1):
+                    for i, s in enumerate((a, b)):
+                        nc.scalar.copy(
+                            out=out_sb[s][:, BANK * n : BANK * (n + 1)], in_=group(n, quantised[i], 0, BANK)[:]
+                        )
                 turn_h()
-                early_sums.append(base_passes(1, quantised))
+                for n in (0, 1):
+                    for s in (a, b):
+                        cols = slice(BANK * n, BANK * (n + 1))
+                        nc.vector.scalar_tensor_tensor(
+                            out=out_sb[s][:, cols],
+                            in0=lora_product(s, n)[:],
+                            scalar=LORA_GAIN,
+                            in1=out_sb[s][:, cols],
+                            op0=MULT,
+                            op1=ADD,
+                        )
+                        store(s, cols)
+                        lora_first(s, n + 2)
+            else:
+                for n in (0, 1):
+                    lora_first(a, n)
+                    lora_first(b, n)
+                    block(a, n, quantised[0])
+                    block(b, n, quantised[1])
             if more:
-                sorted_next = [sort_x(s) for s in (2 * pair + 2, 2 * pair + 3)]
-            for n in (0, 1):
-                lora_products(pair, n)
-                add_and_store(pair, n, early_sums[n] if pair == 0 else base_passes(n, quantised))
+                sorted_next = [sort_x(a + 2), sort_x(b + 2)]
+            if pair > 0:
+                lora_first(a, 2)
+                lora_first(b, 2)
+            block(a, 2, quantised[0])
+            if pair > 0:
+                lora_first(a, 3)
+                lora_first(b, 3)
+            block(b, 2, quantised[1])
             if more:
-                grouped = [turn_x(sorted_next[0])]
-            lora_products(pair, 2)
-            add_and_store(pair, 2, base_passes(2, quantised))
+                grouped_next = [new_grouped(), new_grouped()]
+                for i in (0, 1):
+                    for two in range(PASSES // 2):
+                        turn_two_passes(sorted_next[i][:], True, two, grouped_next[i])
+                quantised_next = [new_quantised(), new_quantised()]
+            sum_a = group(3, quantised[0], 0, BANK)
             if more:
-                grouped.append(turn_x(sorted_next[1]))
-            lora_products(pair, 3)
-            last_sums = base_passes(3, quantised)
+                quantise(grouped_next[0], quantised_next[0], 0, PASSES)
+            add_and_store(a, 3, sum_a, 0, BANK)
+            if more or not TAIL_SPLIT:
+                sum_b = group(3, quantised[1], 0, BANK)
+                if more:
+                    quantise(grouped_next[1], quantised_next[1], 0, PASSES)
+                add_and_store(b, 3, sum_b, 0, BANK)
+            else:
+                for first_col in range(0, BANK, P):
+                    add_and_store(b, 3, group(3, quantised[1], first_col, P), first_col, P)
             if more:
-                quantised = [quantise_x(grouped_x) for grouped_x in grouped]
-            add_and_store(pair, 3, last_sums)
+                quantised = quantised_next

@@ -24,7 +24,7 @@ BLOCKS = OUT_F // BANK
 LORA_GAIN = 2.0
 
 TAIL_SPLIT = False
-DUMMIES = 0
+DUMMIES_FRONT, DUMMIES_MID, DUMMIES_BACK = 0, 0, 0
 
 FLOPS = 2 * ROWS * IN_F * OUT_F + 2 * ROWS * P * OUT_F
 
@@ -44,11 +44,13 @@ def tile_lorasequential_pa_kernel(tc, x, h_lora, lora_B, M_words, M_scales, out)
         out_sb = [resident.tile([P, OUT_F], F32, name="out_sb%d" % s) for s in range(SEGMENTS)]
         h_sb = resident.tile([P, SEGMENTS, P], BF16)
         hT_sb = resident.tile([P, ROWS], BF16)
-        m_words = resident.tile([P, BLOCKS, PASSES, 2 * BANK], U8, align_bytes=64)
-        m_scales = resident.tile([P, BLOCKS, PASSES, BANK], U8, align_bytes=64)
+        m_words = [resident.tile([P, PASSES, 2 * BANK], U8, align_bytes=64, name="m_words%d" % n) for n in range(BLOCKS)]
+        m_scales = [resident.tile([P, PASSES, BANK], U8, align_bytes=64, name="m_scales%d" % n) for n in range(BLOCKS)]
         ident_f32 = resident.tile([P, P], F32)
         ident_bf16 = resident.tile([P, P], BF16)
 
+        zeros = resident.tile([P, BANK], BF16)
+        nc.vector.memset(zeros[:], 0.0)
         make_identity(nc, ident_f32[:])
         make_identity(nc, ident_bf16[:])
 
@@ -57,7 +59,7 @@ def tile_lorasequential_pa_kernel(tc, x, h_lora, lora_B, M_words, M_scales, out)
         nc.scalar.mul(out=warm[:], in_=warm[:], mul=LORA_GAIN)
 
         for n in range(BLOCKS):
-            nc.vector.memset(m_scales[:, n, :, :].rearrange("p g c -> p (g c)").bitcast(I32), 0)
+            nc.vector.memset(m_scales[n][:].rearrange("p g c -> p (g c)").bitcast(I32), 0)
 
         def load_x(s, pieces):
             width = IN_F // pieces
@@ -77,7 +79,7 @@ def tile_lorasequential_pa_kernel(tc, x, h_lora, lora_B, M_words, M_scales, out)
             cols = slice(BANK * n, BANK * (n + 1))
             for r in range(4):
                 nc.sync.dma_start(
-                    out=m_scales[r:P:32, n, :, :].bitcast(I32),
+                    out=m_scales[n][r:P:32, :, :].bitcast(I32),
                     in_=M_scales[:, r:16:4, cols].rearrange("g q c -> q g c").bitcast(I32),
                 )
             byte_cols = slice(2 * BANK * n, 2 * BANK * (n + 1))
@@ -85,12 +87,12 @@ def tile_lorasequential_pa_kernel(tc, x, h_lora, lora_B, M_words, M_scales, out)
             for piece in range(pieces):
                 some = slice(count * piece, count * (piece + 1))
                 nc.sync.dma_start(
-                    out=m_words[:, n, some, :].bitcast(I32),
+                    out=m_words[n][:, some, :].bitcast(I32),
                     in_=M_words[some, :, byte_cols].rearrange("g p c -> p g c").bitcast(I32),
                 )
 
         load_x(0, 2)
-        load_x(1, 2)
+        load_x(1, 1)
         load_m_block(0, 2)
         load_m_block(1, 1)
         load_h()
@@ -156,8 +158,11 @@ def tile_lorasequential_pa_kernel(tc, x, h_lora, lora_B, M_words, M_scales, out)
                 out=hT_sb[:].rearrange("r (p j) -> r p j", j=SEGMENTS), in_=hT_ps[:].rearrange("r j p -> r p j")
             )
 
-        def lora_product(s, n):
-            low_rank = lora_pool.tile([P, BANK], F32, tag="low_rank")
+        def lora_product(s, n, in_turned_bank=False):
+            if in_turned_bank:
+                low_rank = turned_pool.tile([P, BANK], F32, tag="turned")
+            else:
+                low_rank = lora_pool.tile([P, BANK], F32, tag="low_rank")
             nc.tensor.matmul(
                 out=low_rank[:],
                 lhsT=hT_sb[:, P * s : P * (s + 1)],
@@ -167,8 +172,10 @@ def tile_lorasequential_pa_kernel(tc, x, h_lora, lora_B, M_words, M_scales, out)
             )
             return low_rank
 
-        def lora_first(s, n):
-            nc.scalar.mul(out=out_sb[s][:, BANK * n : BANK * (n + 1)], in_=lora_product(s, n)[:], mul=LORA_GAIN)
+        def lora_first(s, n, in_turned_bank=False):
+            nc.scalar.mul(
+                out=out_sb[s][:, BANK * n : BANK * (n + 1)], in_=lora_product(s, n, in_turned_bank)[:], mul=LORA_GAIN
+            )
 
         def group(n, quantised, first_col, width):
             codes, scales = quantised
@@ -179,8 +186,8 @@ def tile_lorasequential_pa_kernel(tc, x, h_lora, lora_B, M_words, M_scales, out)
                     out=base_sum[:, 0:width],
                     lhsT=codes[:, rows].bitcast(FP8X4),
                     lhsT_scale=scales[:, rows],
-                    rhs=m_words[:, n, g, 2 * first_col : 2 * (first_col + width)].bitcast(FP4X4),
-                    rhs_scale=m_scales[:, n, g, first_col : first_col + width],
+                    rhs=m_words[n][:, g, 2 * first_col : 2 * (first_col + width)].bitcast(FP4X4),
+                    rhs_scale=m_scales[n][:, g, first_col : first_col + width],
                     start=(g == 0),
                     stop=(g == PASSES - 1),
                 )
@@ -197,24 +204,19 @@ def tile_lorasequential_pa_kernel(tc, x, h_lora, lora_B, M_words, M_scales, out)
         def block(s, n, quantised):
             add_and_store(s, n, group(n, quantised, 0, BANK), 0, BANK)
 
-        if DUMMIES:
-            zeros = resident.tile([P, BANK], BF16)
-            nc.gpsimd.memset(zeros[:], 0.0)
-
         def dummies(count):
             for i in range(count):
                 idle = lora_pool.tile([P, BANK], F32, tag="low_rank")
                 nc.tensor.matmul(out=idle[:], lhsT=zeros[:, 0:P], rhs=zeros[:], start=True, stop=True)
 
-        if DUMMIES:
-            dummies(DUMMIES)
-
+        dummies(DUMMIES_FRONT)
         quantised = []
         for s in (0, 1):
             grouped = new_grouped()
             fresh = new_quantised()
             for two in range(PASSES // 2):
                 turn_two_passes(x_sb[s][:].bitcast(F32), False, two, grouped)
+                dummies(DUMMIES_BACK if (s, two) == (1, 1) else DUMMIES_MID)
                 quantise(grouped, fresh, 2 * two, 2)
             quantised.append(fresh)
 
@@ -224,23 +226,26 @@ def tile_lorasequential_pa_kernel(tc, x, h_lora, lora_B, M_words, M_scales, out)
             if pair == 0:
                 for n in (0, 1):
                     for i, s in enumerate((a, b)):
+                        if (n, i) == (1, 1):
+                            turn_h()
                         nc.scalar.copy(
                             out=out_sb[s][:, BANK * n : BANK * (n + 1)], in_=group(n, quantised[i], 0, BANK)[:]
                         )
-                turn_h()
+                spare = [False, False, True, True, True, False, False, True]
                 for n in (0, 1):
                     for s in (a, b):
                         cols = slice(BANK * n, BANK * (n + 1))
+                        turn = 2 * (2 * n + s)
                         nc.vector.scalar_tensor_tensor(
                             out=out_sb[s][:, cols],
-                            in0=lora_product(s, n)[:],
+                            in0=lora_product(s, n, spare[turn])[:],
                             scalar=LORA_GAIN,
                             in1=out_sb[s][:, cols],
                             op0=MULT,
                             op1=ADD,
                         )
                         store(s, cols)
-                        lora_first(s, n + 2)
+                        lora_first(s, n + 2, spare[turn + 1])
             else:
                 for n in (0, 1):
                     lora_first(a, n)

@@ -23,8 +23,10 @@ BANK = 512
 BLOCKS = OUT_F // BANK
 LORA_GAIN = 2.0
 
-TAIL_SPLIT = False
+TAIL_SPLIT = True
 DUMMIES_FRONT, DUMMIES_MID, DUMMIES_BACK = 0, 0, 0
+VECTOR_PAIRS = (2, 3)
+Q = 32
 
 FLOPS = 2 * ROWS * IN_F * OUT_F + 2 * ROWS * P * OUT_F
 
@@ -39,7 +41,11 @@ def tile_lorasequential_pa_kernel(tc, x, h_lora, lora_B, M_words, M_scales, out)
         base_pool = stack.enter_context(tc.psum_pool(name="base_pool", bufs=3))
         stack.enter_context(tc.manual_schedule())
 
-        x_sb = [resident.tile([P, IN_F], BF16, name="x_sb%d" % s) for s in range(SEGMENTS)]
+        x_sb = [resident.tile([P, IN_F], BF16, name="x_sb%d" % s) for s in range(SEGMENTS) if s // 2 not in VECTOR_PAIRS]
+        landed = dict(
+            (pair, resident.tile([P, PASSES, 2 * P // Q, P], BF16, name="landed%d" % pair)) for pair in VECTOR_PAIRS
+        )
+        turning = stack.enter_context(tc.tile_pool(name="turning", bufs=1))
         b_sb = [resident.tile([P, OUT_F], BF16, name="b_sb%d" % s) for s in range(SEGMENTS)]
         out_sb = [resident.tile([P, OUT_F], F32, name="out_sb%d" % s) for s in range(SEGMENTS)]
         h_sb = resident.tile([P, SEGMENTS, P], BF16)
@@ -66,6 +72,15 @@ def tile_lorasequential_pa_kernel(tc, x, h_lora, lora_B, M_words, M_scales, out)
             for piece in range(pieces):
                 cols = slice(width * piece, width * (piece + 1))
                 nc.sync.dma_start(out=x_sb[s][:, cols], in_=x[P * s : P * (s + 1), cols])
+
+        def load_x_by_quadrants(pair):
+            for g in range(PASSES):
+                for c in range(P // Q):
+                    first = K_PASS * g + P * c
+                    nc.sync.dma_start(
+                        out=landed[pair][Q * c : Q * (c + 1), g, :, :],
+                        in_=x[2 * P * pair : 2 * P * (pair + 1), first : first + P].rearrange("(R q) e -> q R e", q=Q),
+                    )
 
         def load_lora_b(s):
             nc.sync.dma_start(out=b_sb[s][:], in_=lora_B[s])
@@ -105,7 +120,9 @@ def tile_lorasequential_pa_kernel(tc, x, h_lora, lora_B, M_words, M_scales, out)
         for pair in range(1, PAIRS):
             load_lora_b(2 * pair)
             load_lora_b(2 * pair + 1)
-            if pair + 1 < PAIRS:
+            if pair + 1 in VECTOR_PAIRS:
+                load_x_by_quadrants(pair + 1)
+            elif pair + 1 < PAIRS:
                 load_x(2 * pair + 2, 1)
                 load_x(2 * pair + 3, 1)
 
@@ -130,6 +147,30 @@ def tile_lorasequential_pa_kernel(tc, x, h_lora, lora_B, M_words, M_scales, out)
             nc.scalar.copy(
                 out=grouped_words[:, 2 * two : 2 * two + 2, :, :],
                 in_=turned[:].rearrange("p (g u) r -> p g r u", u=2),
+            )
+
+        def turn_by_vector(pair):
+            parted = turning.tile([P, IN_F], F32, align_bytes=64, tag="parted")
+            turned_words = turning.tile([P, IN_F], F32, align_bytes=64, tag="turned_words")
+            half = IN_F // 2
+            for two in range(PASSES // 2):
+                cols = slice(half * two, half * (two + 1))
+                nc.vector.tensor_copy(
+                    out=parted[:, cols].rearrange("r (j u c) -> r j u c", u=2, c=Q),
+                    in_=landed[pair][:, 2 * two : 2 * two + 2, :, :]
+                    .rearrange("r g R e -> r (g R e)")
+                    .bitcast(F32)
+                    .rearrange("r (j c u) -> r j u c", u=2, c=Q),
+                )
+                nc.vector.transpose(out=turned_words[:, cols], in_=parted[:, cols])
+            return turned_words
+
+        def group_words(turned_words, i, g, grouped):
+            nc.scalar.copy(
+                out=grouped[:].bitcast(F32).rearrange("p (g R q u) -> p g R q u", g=PASSES, q=Q, u=2)[:, g, :, :, :],
+                in_=turned_words[:].rearrange("p (g R u q) -> p g R q u", g=PASSES, u=2, q=Q)[
+                    :, g, P // Q * i : P // Q * (i + 1), :, :
+                ],
             )
 
         def new_grouped():
@@ -177,9 +218,12 @@ def tile_lorasequential_pa_kernel(tc, x, h_lora, lora_B, M_words, M_scales, out)
                 out=out_sb[s][:, BANK * n : BANK * (n + 1)], in_=lora_product(s, n, in_turned_bank)[:], mul=LORA_GAIN
             )
 
-        def group(n, quantised, first_col, width):
+        def group(n, quantised, first_col, width, in_turned_bank=False):
             codes, scales = quantised
-            base_sum = base_pool.tile([P, BANK], F32, tag="base_sum")
+            if in_turned_bank:
+                base_sum = turned_pool.tile([P, BANK], F32, tag="turned")
+            else:
+                base_sum = base_pool.tile([P, BANK], F32, tag="base_sum")
             for g in range(PASSES):
                 rows = slice(P * g, P * (g + 1))
                 nc.tensor.matmul_mx(
@@ -201,8 +245,8 @@ def tile_lorasequential_pa_kernel(tc, x, h_lora, lora_B, M_words, M_scales, out)
             nc.vector.tensor_tensor(out=out_sb[s][:, cols], in0=base_sum[:, 0:width], in1=out_sb[s][:, cols], op=ADD)
             store(s, cols)
 
-        def block(s, n, quantised):
-            add_and_store(s, n, group(n, quantised, 0, BANK), 0, BANK)
+        def block(s, n, quantised, in_turned_bank=False):
+            add_and_store(s, n, group(n, quantised, 0, BANK, in_turned_bank), 0, BANK)
 
         def dummies(count):
             for i in range(count):
@@ -223,6 +267,8 @@ def tile_lorasequential_pa_kernel(tc, x, h_lora, lora_B, M_words, M_scales, out)
         for pair in range(PAIRS):
             a, b = 2 * pair, 2 * pair + 1
             more = pair + 1 < PAIRS
+            by_vector = pair + 1 in VECTOR_PAIRS
+            spare = pair > 0 and all(later in VECTOR_PAIRS for later in range(pair + 1, PAIRS))
             if pair == 0:
                 for n in (0, 1):
                     for i, s in enumerate((a, b)):
@@ -247,38 +293,55 @@ def tile_lorasequential_pa_kernel(tc, x, h_lora, lora_B, M_words, M_scales, out)
                         store(s, cols)
                         lora_first(s, n + 2, spare[turn + 1])
             else:
-                for n in (0, 1):
-                    lora_first(a, n)
-                    lora_first(b, n)
-                    block(a, n, quantised[0])
-                    block(b, n, quantised[1])
-            if more:
+                lora_first(a, 0)
+                lora_first(b, 0)
+                block(a, 0, quantised[0])
+                block(b, 0, quantised[1], spare)
+                if by_vector:
+                    turned_words = turn_by_vector(pair + 1)
+                    grouped_next = [new_grouped(), new_grouped()]
+                lora_first(a, 1)
+                lora_first(b, 1)
+                block(a, 1, quantised[0])
+                block(b, 1, quantised[1], spare)
+                if by_vector:
+                    for i in (0, 1):
+                        for g in (0, 1):
+                            group_words(turned_words, i, g, grouped_next[i])
+            if more and not by_vector:
                 sorted_next = [sort_x(a + 2), sort_x(b + 2)]
             if pair > 0:
                 lora_first(a, 2)
                 lora_first(b, 2)
             block(a, 2, quantised[0])
-            if pair > 0:
+            if pair > 0 and not by_vector:
                 lora_first(a, 3)
                 lora_first(b, 3)
-            block(b, 2, quantised[1])
-            if more:
+            block(b, 2, quantised[1], spare)
+            if by_vector:
+                for i in (0, 1):
+                    for g in (2, 3):
+                        group_words(turned_words, i, g, grouped_next[i])
+                lora_first(a, 3)
+                lora_first(b, 3)
+            elif more:
                 grouped_next = [new_grouped(), new_grouped()]
                 for i in (0, 1):
                     for two in range(PASSES // 2):
                         turn_two_passes(sorted_next[i][:], True, two, grouped_next[i])
+            if more:
                 quantised_next = [new_quantised(), new_quantised()]
             sum_a = group(3, quantised[0], 0, BANK)
             if more:
                 quantise(grouped_next[0], quantised_next[0], 0, PASSES)
             add_and_store(a, 3, sum_a, 0, BANK)
             if more or not TAIL_SPLIT:
-                sum_b = group(3, quantised[1], 0, BANK)
+                sum_b = group(3, quantised[1], 0, BANK, spare)
                 if more:
                     quantise(grouped_next[1], quantised_next[1], 0, PASSES)
                 add_and_store(b, 3, sum_b, 0, BANK)
             else:
                 for first_col in range(0, BANK, P):
-                    add_and_store(b, 3, group(3, quantised[1], first_col, P), first_col, P)
+                    add_and_store(b, 3, group(3, quantised[1], first_col, P, first_col % (2 * P) > 0), first_col, P)
             if more:
                 quantised = quantised_next

@@ -24,7 +24,6 @@ BLOCKS = OUT_F // BANK
 LORA_GAIN = 2.0
 
 TAIL_SPLIT = True
-DUMMIES_FRONT, DUMMIES_MID, DUMMIES_BACK = 0, 0, 0
 VECTOR_PAIRS = (2, 3)
 Q = 32
 
@@ -55,8 +54,6 @@ def tile_lorasequential_pa_kernel(tc, x, h_lora, lora_B, M_words, M_scales, out)
         ident_f32 = resident.tile([P, P], F32)
         ident_bf16 = resident.tile([P, P], BF16)
 
-        zeros = resident.tile([P, BANK], BF16)
-        nc.vector.memset(zeros[:], 0.0)
         make_identity(nc, ident_f32[:])
         make_identity(nc, ident_bf16[:])
 
@@ -109,22 +106,19 @@ def tile_lorasequential_pa_kernel(tc, x, h_lora, lora_B, M_words, M_scales, out)
         load_x(0, 2)
         load_x(1, 1)
         load_m_block(0, 2)
-        load_m_block(1, 1)
+        for n in range(1, BLOCKS):
+            load_m_block(n, 1)
+        load_x(2, 1)
+        load_x(3, 1)
         load_h()
         load_lora_b(0)
         load_lora_b(1)
-        load_m_block(2, 1)
-        load_x(2, 1)
-        load_x(3, 1)
-        load_m_block(3, 1)
-        for pair in range(1, PAIRS):
-            load_lora_b(2 * pair)
-            load_lora_b(2 * pair + 1)
-            if pair + 1 in VECTOR_PAIRS:
-                load_x_by_quadrants(pair + 1)
-            elif pair + 1 < PAIRS:
-                load_x(2 * pair + 2, 1)
-                load_x(2 * pair + 3, 1)
+        load_x_by_quadrants(2)
+        load_lora_b(2)
+        load_lora_b(3)
+        load_x_by_quadrants(3)
+        for s in range(4, SEGMENTS):
+            load_lora_b(s)
 
         def sort_x(s):
             sorted_words = operand.tile([P, IN_F // 2], F32, tag="sorted_words")
@@ -134,7 +128,7 @@ def tile_lorasequential_pa_kernel(tc, x, h_lora, lora_B, M_words, M_scales, out)
             )
             return sorted_words
 
-        def turn_two_passes(words, is_sorted, two, grouped):
+        def turn_two_passes(words, is_sorted, two, grouped, by_vector=False):
             turned = turned_pool.tile([P, 4, P], F32, tag="turned")
             for j in range(4):
                 if is_sorted:
@@ -144,10 +138,16 @@ def tile_lorasequential_pa_kernel(tc, x, h_lora, lora_B, M_words, M_scales, out)
                     source = words[:, 2 * P * g + u : 2 * P * (g + 1) : 2]
                 nc.tensor.transpose(turned[:, j, :], source, ident_f32[:])
             grouped_words = grouped[:].bitcast(F32).rearrange("p (g r u) -> p g r u", r=P, u=2)
-            nc.scalar.copy(
-                out=grouped_words[:, 2 * two : 2 * two + 2, :, :],
-                in_=turned[:].rearrange("p (g u) r -> p g r u", u=2),
-            )
+            if by_vector:
+                nc.vector.tensor_copy(
+                    out=grouped_words[:, 2 * two : 2 * two + 2, :, :],
+                    in_=turned[:].rearrange("p (g u) r -> p g r u", u=2),
+                )
+            else:
+                nc.scalar.copy(
+                    out=grouped_words[:, 2 * two : 2 * two + 2, :, :],
+                    in_=turned[:].rearrange("p (g u) r -> p g r u", u=2),
+                )
 
         def turn_by_vector(pair):
             parted = turning.tile([P, IN_F], F32, align_bytes=64, tag="parted")
@@ -245,22 +245,30 @@ def tile_lorasequential_pa_kernel(tc, x, h_lora, lora_B, M_words, M_scales, out)
             nc.vector.tensor_tensor(out=out_sb[s][:, cols], in0=base_sum[:, 0:width], in1=out_sb[s][:, cols], op=ADD)
             store(s, cols)
 
+        def base_first(s, n, quantised):
+            nc.scalar.copy(out=out_sb[s][:, BANK * n : BANK * (n + 1)], in_=group(n, quantised, 0, BANK)[:])
+
+        def lora_second(s, n, in_turned_bank):
+            cols = slice(BANK * n, BANK * (n + 1))
+            nc.vector.scalar_tensor_tensor(
+                out=out_sb[s][:, cols],
+                in0=lora_product(s, n, in_turned_bank)[:],
+                scalar=LORA_GAIN,
+                in1=out_sb[s][:, cols],
+                op0=MULT,
+                op1=ADD,
+            )
+            store(s, cols)
+
         def block(s, n, quantised, in_turned_bank=False):
             add_and_store(s, n, group(n, quantised, 0, BANK, in_turned_bank), 0, BANK)
 
-        def dummies(count):
-            for i in range(count):
-                idle = lora_pool.tile([P, BANK], F32, tag="low_rank")
-                nc.tensor.matmul(out=idle[:], lhsT=zeros[:, 0:P], rhs=zeros[:], start=True, stop=True)
-
-        dummies(DUMMIES_FRONT)
         quantised = []
         for s in (0, 1):
             grouped = new_grouped()
             fresh = new_quantised()
             for two in range(PASSES // 2):
                 turn_two_passes(x_sb[s][:].bitcast(F32), False, two, grouped)
-                dummies(DUMMIES_BACK if (s, two) == (1, 1) else DUMMIES_MID)
                 quantise(grouped, fresh, 2 * two, 2)
             quantised.append(fresh)
 
@@ -268,80 +276,43 @@ def tile_lorasequential_pa_kernel(tc, x, h_lora, lora_B, M_words, M_scales, out)
             a, b = 2 * pair, 2 * pair + 1
             more = pair + 1 < PAIRS
             by_vector = pair + 1 in VECTOR_PAIRS
-            spare = pair > 0 and all(later in VECTOR_PAIRS for later in range(pair + 1, PAIRS))
-            if pair == 0:
-                for n in (0, 1):
-                    for i, s in enumerate((a, b)):
-                        if (n, i) == (1, 1):
-                            turn_h()
-                        nc.scalar.copy(
-                            out=out_sb[s][:, BANK * n : BANK * (n + 1)], in_=group(n, quantised[i], 0, BANK)[:]
-                        )
-                spare = [False, False, True, True, True, False, False, True]
-                for n in (0, 1):
-                    for s in (a, b):
-                        cols = slice(BANK * n, BANK * (n + 1))
-                        turn = 2 * (2 * n + s)
-                        nc.vector.scalar_tensor_tensor(
-                            out=out_sb[s][:, cols],
-                            in0=lora_product(s, n, spare[turn])[:],
-                            scalar=LORA_GAIN,
-                            in1=out_sb[s][:, cols],
-                            op0=MULT,
-                            op1=ADD,
-                        )
-                        store(s, cols)
-                        lora_first(s, n + 2, spare[turn + 1])
-            else:
-                lora_first(a, 0)
-                lora_first(b, 0)
-                block(a, 0, quantised[0])
-                block(b, 0, quantised[1], spare)
-                if by_vector:
+            for n in range(BLOCKS):
+                if pair > 0:
+                    lora_second(a - 2, n, False)
+                    lora_second(b - 2, n, True)
+                if not more:
+                    lora_first(a, n, True)
+                    lora_first(b, n, True)
+                if n == BLOCKS - 1 and more and not by_vector:
+                    grouped_next = [new_grouped(), new_grouped()]
+                    for i in (0, 1):
+                        for two in range(PASSES // 2):
+                            turn_two_passes(sorted_next[i][:], True, two, grouped_next[i], two == 1)
+                    turn_h()
+                if n == BLOCKS - 1 and more:
+                    quantised_next = [new_quantised(), new_quantised()]
+                if more:
+                    base_first(a, n, quantised[0])
+                    if n == BLOCKS - 1:
+                        quantise(grouped_next[0], quantised_next[0], 0, PASSES)
+                    base_first(b, n, quantised[1])
+                    if n == BLOCKS - 1:
+                        quantise(grouped_next[1], quantised_next[1], 0, PASSES)
+                else:
+                    block(a, n, quantised[0])
+                    if n < BLOCKS - 1 or not TAIL_SPLIT:
+                        block(b, n, quantised[1])
+                    else:
+                        for first_col in range(0, BANK, P):
+                            add_and_store(b, n, group(n, quantised[1], first_col, P), first_col, P)
+                if n == 0 and more and not by_vector:
+                    sorted_next = [sort_x(a + 2), sort_x(b + 2)]
+                if n == 0 and by_vector:
                     turned_words = turn_by_vector(pair + 1)
                     grouped_next = [new_grouped(), new_grouped()]
-                lora_first(a, 1)
-                lora_first(b, 1)
-                block(a, 1, quantised[0])
-                block(b, 1, quantised[1], spare)
-                if by_vector:
+                if n in (1, 2) and by_vector:
                     for i in (0, 1):
-                        for g in (0, 1):
+                        for g in (2 * n - 2, 2 * n - 1):
                             group_words(turned_words, i, g, grouped_next[i])
-            if more and not by_vector:
-                sorted_next = [sort_x(a + 2), sort_x(b + 2)]
-            if pair > 0:
-                lora_first(a, 2)
-                lora_first(b, 2)
-            block(a, 2, quantised[0])
-            if pair > 0 and not by_vector:
-                lora_first(a, 3)
-                lora_first(b, 3)
-            block(b, 2, quantised[1], spare)
-            if by_vector:
-                for i in (0, 1):
-                    for g in (2, 3):
-                        group_words(turned_words, i, g, grouped_next[i])
-                lora_first(a, 3)
-                lora_first(b, 3)
-            elif more:
-                grouped_next = [new_grouped(), new_grouped()]
-                for i in (0, 1):
-                    for two in range(PASSES // 2):
-                        turn_two_passes(sorted_next[i][:], True, two, grouped_next[i])
-            if more:
-                quantised_next = [new_quantised(), new_quantised()]
-            sum_a = group(3, quantised[0], 0, BANK)
-            if more:
-                quantise(grouped_next[0], quantised_next[0], 0, PASSES)
-            add_and_store(a, 3, sum_a, 0, BANK)
-            if more or not TAIL_SPLIT:
-                sum_b = group(3, quantised[1], 0, BANK, spare)
-                if more:
-                    quantise(grouped_next[1], quantised_next[1], 0, PASSES)
-                add_and_store(b, 3, sum_b, 0, BANK)
-            else:
-                for first_col in range(0, BANK, P):
-                    add_and_store(b, 3, group(3, quantised[1], first_col, P, first_col % (2 * P) > 0), first_col, P)
             if more:
                 quantised = quantised_next

@@ -104,7 +104,7 @@ def tile_lorasequential_pa_kernel(tc, x, h_lora, lora_B, M_words, M_scales, out)
                 )
 
         load_x(0, 2)
-        load_x(1, 1)
+        load_x(1, 2)
         load_m_block(0, 2)
         for n in range(1, BLOCKS):
             load_m_block(n, 1)
@@ -120,12 +120,15 @@ def tile_lorasequential_pa_kernel(tc, x, h_lora, lora_B, M_words, M_scales, out)
         for s in range(4, SEGMENTS):
             load_lora_b(s)
 
-        def sort_x(s):
+        def sort_x(s, pieces=1):
             sorted_words = operand.tile([P, IN_F // 2], F32, tag="sorted_words")
-            nc.vector.tensor_copy(
-                out=sorted_words[:].rearrange("r (g u p) -> r g u p", u=2, p=P),
-                in_=x_sb[s][:].bitcast(F32).rearrange("r (g p u) -> r g u p", u=2, p=P),
-            )
+            width = IN_F // 2 // pieces
+            for piece in range(pieces):
+                cols = slice(width * piece, width * (piece + 1))
+                nc.vector.tensor_copy(
+                    out=sorted_words[:, cols].rearrange("r (g u p) -> r g u p", u=2, p=P),
+                    in_=x_sb[s][:].bitcast(F32)[:, cols].rearrange("r (g p u) -> r g u p", u=2, p=P),
+                )
             return sorted_words
 
         def turn_two_passes(words, is_sorted, two, grouped, by_vector=False):
@@ -264,11 +267,12 @@ def tile_lorasequential_pa_kernel(tc, x, h_lora, lora_B, M_words, M_scales, out)
             add_and_store(s, n, group(n, quantised, 0, BANK, in_turned_bank), 0, BANK)
 
         quantised = []
+        sorted_first = [sort_x(s, 2) for s in (0, 1)]
         for s in (0, 1):
             grouped = new_grouped()
             fresh = new_quantised()
             for two in range(PASSES // 2):
-                turn_two_passes(x_sb[s][:].bitcast(F32), False, two, grouped)
+                turn_two_passes(sorted_first[s][:], True, two, grouped)
                 quantise(grouped, fresh, 2 * two, 2)
             quantised.append(fresh)
 

@@ -105,12 +105,12 @@ def tile_lorasequential_pa_kernel(tc, x, h_lora, lora_B, M_words, M_scales, out)
 
         load_x(0, 2)
         load_x(1, 2)
+        load_h()
         load_m_block(0, 2)
         for n in range(1, BLOCKS):
             load_m_block(n, 1)
         load_x(2, 1)
         load_x(3, 1)
-        load_h()
         load_lora_b(0)
         load_lora_b(1)
         load_x_by_quadrants(2)
@@ -275,6 +275,7 @@ def tile_lorasequential_pa_kernel(tc, x, h_lora, lora_B, M_words, M_scales, out)
                 turn_two_passes(sorted_first[s][:], True, two, grouped)
                 quantise(grouped, fresh, 2 * two, 2)
             quantised.append(fresh)
+        turn_h()
 
         for pair in range(PAIRS):
             a, b = 2 * pair, 2 * pair + 1
@@ -292,7 +293,6 @@ def tile_lorasequential_pa_kernel(tc, x, h_lora, lora_B, M_words, M_scales, out)
                     for i in (0, 1):
                         for two in range(PASSES // 2):
                             turn_two_passes(sorted_next[i][:], True, two, grouped_next[i], two == 1)
-                    turn_h()
                 if n == BLOCKS - 1 and more:
                     quantised_next = [new_quantised(), new_quantised()]
                 if more:

@@ -288,20 +288,18 @@ def tile_lorasequential_pa_kernel(tc, x, h_lora, lora_B, M_words, M_scales, out)
                 if not more:
                     lora_first(a, n, True)
                     lora_first(b, n, True)
-                if n == BLOCKS - 1 and more and not by_vector:
-                    grouped_next = [new_grouped(), new_grouped()]
-                    for i in (0, 1):
-                        for two in range(PASSES // 2):
-                            turn_two_passes(sorted_next[i][:], True, two, grouped_next[i], two == 1)
                 if n == BLOCKS - 1 and more:
                     quantised_next = [new_quantised(), new_quantised()]
+                if n == BLOCKS - 1 and more and not by_vector:
+                    grouped_next = [new_grouped(), new_grouped()]
                 if more:
-                    base_first(a, n, quantised[0])
-                    if n == BLOCKS - 1:
-                        quantise(grouped_next[0], quantised_next[0], 0, PASSES)
-                    base_first(b, n, quantised[1])
-                    if n == BLOCKS - 1:
-                        quantise(grouped_next[1], quantised_next[1], 0, PASSES)
+                    for i, s in ((0, a), (1, b)):
+                        base_first(s, n, quantised[i])
+                        if n == BLOCKS - 1:
+                            if not by_vector:
+                                for two in range(PASSES // 2):
+                                    turn_two_passes(sorted_next[i][:], True, two, grouped_next[i], two == 1)
+                            quantise(grouped_next[i], quantised_next[i], 0, PASSES)
                 else:
                     block(a, n, quantised[0])
                     if n < BLOCKS - 1 or not TAIL_SPLIT:

@@ -152,21 +152,17 @@ def tile_lorasequential_pa_kernel(tc, x, h_lora, lora_B, M_words, M_scales, out)
                     in_=turned[:].rearrange("p (g u) r -> p g r u", u=2),
                 )
 
-        def turn_by_vector(pair):
-            parted = turning.tile([P, IN_F], F32, align_bytes=64, tag="parted")
-            turned_words = turning.tile([P, IN_F], F32, align_bytes=64, tag="turned_words")
+        def turn_by_vector(pair, two, parted, turned_words):
             half = IN_F // 2
-            for two in range(PASSES // 2):
-                cols = slice(half * two, half * (two + 1))
-                nc.vector.tensor_copy(
-                    out=parted[:, cols].rearrange("r (j u c) -> r j u c", u=2, c=Q),
-                    in_=landed[pair][:, 2 * two : 2 * two + 2, :, :]
-                    .rearrange("r g R e -> r (g R e)")
-                    .bitcast(F32)
-                    .rearrange("r (j c u) -> r j u c", u=2, c=Q),
-                )
-                nc.vector.transpose(out=turned_words[:, cols], in_=parted[:, cols])
-            return turned_words
+            cols = slice(half * two, half * (two + 1))
+            nc.vector.tensor_copy(
+                out=parted[:, cols].rearrange("r (j u c) -> r j u c", u=2, c=Q),
+                in_=landed[pair][:, 2 * two : 2 * two + 2, :, :]
+                .rearrange("r g R e -> r (g R e)")
+                .bitcast(F32)
+                .rearrange("r (j c u) -> r j u c", u=2, c=Q),
+            )
+            nc.vector.transpose(out=turned_words[:, cols], in_=parted[:, cols])
 
         def group_words(turned_words, i, g, grouped):
             nc.scalar.copy(
@@ -309,10 +305,12 @@ def tile_lorasequential_pa_kernel(tc, x, h_lora, lora_B, M_words, M_scales, out)
                             add_and_store(b, n, group(n, quantised[1], first_col, P), first_col, P)
                 if n == 0 and more and not by_vector:
                     sorted_next = [sort_x(a + 2), sort_x(b + 2)]
-                if n == 0 and by_vector:
-                    turned_words = turn_by_vector(pair + 1)
-                    grouped_next = [new_grouped(), new_grouped()]
                 if n in (1, 2) and by_vector:
+                    if n == 1:
+                        parted = turning.tile([P, IN_F], F32, align_bytes=64, tag="parted")
+                        turned_words = turning.tile([P, IN_F], F32, align_bytes=64, tag="turned_words")
+                        grouped_next = [new_grouped(), new_grouped()]
+                    turn_by_vector(pair + 1, n - 1, parted, turned_words)
                     for i in (0, 1):
                         for g in (2 * n - 2, 2 * n - 1):
                             group_words(turned_words, i, g, grouped_next[i])

@@ -72,7 +72,7 @@ def tile_lorasequential_pa_kernel(tc, x, h_lora, lora_B, M_words, M_scales, out)
 
         def load_x_by_quadrants(pair):
             for g in range(PASSES):
-                for c in range(P // Q):
+                for c in (0, 2, 1, 3):
                     first = K_PASS * g + P * c
                     nc.sync.dma_start(
                         out=landed[pair][Q * c : Q * (c + 1), g, :, :],
@@ -239,6 +239,12 @@ def tile_lorasequential_pa_kernel(tc, x, h_lora, lora_B, M_words, M_scales, out)
         def store(s, cols):
             nc.sync.dma_start(out=out[P * s : P * (s + 1), cols], in_=out_sb[s][:, cols])
 
+        def store_two_blocks(s, n):
+            if s >= SEGMENTS - 4 and n >= 2:
+                store(s, slice(BANK * n, BANK * (n + 1)))
+            elif n % 2 == 1:
+                store(s, slice(BANK * (n - 1), BANK * (n + 1)))
+
         def add_and_store(s, n, base_sum, first_col, width):
             cols = slice(BANK * n + first_col, BANK * n + first_col + width)
             nc.vector.tensor_tensor(out=out_sb[s][:, cols], in0=base_sum[:, 0:width], in1=out_sb[s][:, cols], op=ADD)
@@ -257,7 +263,7 @@ def tile_lorasequential_pa_kernel(tc, x, h_lora, lora_B, M_words, M_scales, out)
                 op0=MULT,
                 op1=ADD,
             )
-            store(s, cols)
+            store_two_blocks(s, n)
 
         def block(s, n, quantised, in_turned_bank=False):
             add_and_store(s, n, group(n, quantised, 0, BANK, in_turned_bank), 0, BANK)
@@ -302,7 +308,7 @@ def tile_lorasequential_pa_kernel(tc, x, h_lora, lora_B, M_words, M_scales, out)
                         block(b, n, quantised[1])
                     else:
                         for first_col in range(0, BANK, P):
-                            add_and_store(b, n, group(n, quantised[1], first_col, P), first_col, P)
+                            add_and_store(b, n, group(n, quantised[1], first_col, P, first_col % (2 * P) == P), first_col, P)
                 if n == 0 and more and not by_vector:
                     sorted_next = [sort_x(a + 2), sort_x(b + 2)]
                 if n in (1, 2) and by_vector:

@@ -21,6 +21,8 @@ K_PASS = 4 * P
 PASSES = IN_F // K_PASS
 BANK = 512
 BLOCKS = OUT_F // BANK
+FIRST_EDGES = (0, K_PASS, 2 * K_PASS, IN_F)
+EDGES = (0, 2 * K_PASS, IN_F)
 LORA_GAIN = 2.0
 
 TAIL_SPLIT = True
@@ -64,11 +66,9 @@ def tile_lorasequential_pa_kernel(tc, x, h_lora, lora_B, M_words, M_scales, out)
         for n in range(BLOCKS):
             nc.vector.memset(m_scales[n][:].rearrange("p g c -> p (g c)").bitcast(I32), 0)
 
-        def load_x(s, pieces):
-            width = IN_F // pieces
-            for piece in range(pieces):
-                cols = slice(width * piece, width * (piece + 1))
-                nc.sync.dma_start(out=x_sb[s][:, cols], in_=x[P * s : P * (s + 1), cols])
+        def load_x(s, edges):
+            for first, last in zip(edges[:-1], edges[1:]):
+                nc.sync.dma_start(out=x_sb[s][:, first:last], in_=x[P * s : P * (s + 1), first:last])
 
         def load_x_by_quadrants(pair):
             for g in range(PASSES):
@@ -103,14 +103,14 @@ def tile_lorasequential_pa_kernel(tc, x, h_lora, lora_B, M_words, M_scales, out)
                     in_=M_words[some, :, byte_cols].rearrange("g p c -> p g c").bitcast(I32),
                 )
 
-        load_x(0, 2)
-        load_x(1, 2)
+        load_x(0, FIRST_EDGES)
+        load_x(1, EDGES)
         load_h()
         load_m_block(0, 2)
         for n in range(1, BLOCKS):
             load_m_block(n, 1)
-        load_x(2, 1)
-        load_x(3, 1)
+        load_x(2, (0, IN_F))
+        load_x(3, (0, IN_F))
         load_lora_b(0)
         load_lora_b(1)
         load_x_by_quadrants(2)
@@ -120,11 +120,10 @@ def tile_lorasequential_pa_kernel(tc, x, h_lora, lora_B, M_words, M_scales, out)
         for s in range(4, SEGMENTS):
             load_lora_b(s)
 
-        def sort_x(s, pieces=1):
+        def sort_x(s, edges=(0, IN_F)):
             sorted_words = operand.tile([P, IN_F // 2], F32, tag="sorted_words")
-            width = IN_F // 2 // pieces
-            for piece in range(pieces):
-                cols = slice(width * piece, width * (piece + 1))
+            for first, last in zip(edges[:-1], edges[1:]):
+                cols = slice(first // 2, last // 2)
                 nc.vector.tensor_copy(
                     out=sorted_words[:, cols].rearrange("r (g u p) -> r g u p", u=2, p=P),
                     in_=x_sb[s][:].bitcast(F32)[:, cols].rearrange("r (g p u) -> r g u p", u=2, p=P),
@@ -269,7 +268,7 @@ def tile_lorasequential_pa_kernel(tc, x, h_lora, lora_B, M_words, M_scales, out)
             add_and_store(s, n, group(n, quantised, 0, BANK, in_turned_bank), 0, BANK)
 
         quantised = []
-        sorted_first = [sort_x(s, 2) for s in (0, 1)]
+        sorted_first = [sort_x(0, FIRST_EDGES), sort_x(1, EDGES)]
         for s in (0, 1):
             grouped = new_grouped()
             fresh = new_quantised()
@@ -284,9 +283,10 @@ def tile_lorasequential_pa_kernel(tc, x, h_lora, lora_B, M_words, M_scales, out)
             more = pair + 1 < PAIRS
             by_vector = pair + 1 in VECTOR_PAIRS
             for n in range(BLOCKS):
-                if pair > 0:
-                    lora_second(a - 2, n, False)
-                    lora_second(b - 2, n, True)
+                if pair > 0 and (n % 2 == 0 or not more):
+                    for j in (n, n + 1) if more else (n,):
+                        lora_second(a - 2, j, False)
+                        lora_second(b - 2, j, True)
                 if not more:
                     lora_first(a, n, True)
                     lora_first(b, n, True)
@@ -316,7 +316,8 @@ def tile_lorasequential_pa_kernel(tc, x, h_lora, lora_B, M_words, M_scales, out)
                         parted = turning.tile([P, IN_F], F32, align_bytes=64, tag="parted")
                         turned_words = turning.tile([P, IN_F], F32, align_bytes=64, tag="turned_words")
                         grouped_next = [new_grouped(), new_grouped()]
-                    turn_by_vector(pair + 1, n - 1, parted, turned_words)
+                        for two in range(PASSES // 2):
+                            turn_by_vector(pair + 1, two, parted, turned_words)
                     for i in (0, 1):
                         for g in (2 * n - 2, 2 * n - 1):
                             group_words(turned_words, i, g, grouped_next[i])

@@ -59,6 +59,8 @@ def tile_lorasequential_pa_kernel(tc, x, h_lora, lora_B, M_words, M_scales, out)
         make_identity(nc, ident_f32[:])
         make_identity(nc, ident_bf16[:])
 
+        idle = resident.tile([P, BANK], BF16)
+        nc.vector.memset(idle[:], 0.0)
         warm = resident.tile([P, 1], F32)
         nc.vector.memset(warm[:], 0.0)
         nc.scalar.mul(out=warm[:], in_=warm[:], mul=LORA_GAIN)
@@ -105,8 +107,8 @@ def tile_lorasequential_pa_kernel(tc, x, h_lora, lora_B, M_words, M_scales, out)
 
         load_x(0, FIRST_EDGES)
         load_x(1, EDGES)
-        load_h()
         load_m_block(0, 2)
+        load_h()
         for n in range(1, BLOCKS):
             load_m_block(n, 1)
         load_x(2, (0, IN_F))
@@ -267,6 +269,12 @@ def tile_lorasequential_pa_kernel(tc, x, h_lora, lora_B, M_words, M_scales, out)
         def block(s, n, quantised, in_turned_bank=False):
             add_and_store(s, n, group(n, quantised, 0, BANK, in_turned_bank), 0, BANK)
 
+        def idle_products(count):
+            for n in range(count):
+                unread = lora_pool.tile([P, BANK], F32, tag="low_rank")
+                nc.tensor.matmul(out=unread[:], lhsT=idle[:, 0:P], rhs=idle[:], start=True, stop=True)
+
+        idle_products(4)
         quantised = []
         sorted_first = [sort_x(0, FIRST_EDGES), sort_x(1, EDGES)]
         for s in (0, 1):
@@ -276,7 +284,6 @@ def tile_lorasequential_pa_kernel(tc, x, h_lora, lora_B, M_words, M_scales, out)
                 turn_two_passes(sorted_first[s][:], True, two, grouped)
                 quantise(grouped, fresh, 2 * two, 2)
             quantised.append(fresh)
-        turn_h()
 
         for pair in range(PAIRS):
             a, b = 2 * pair, 2 * pair + 1
@@ -297,6 +304,8 @@ def tile_lorasequential_pa_kernel(tc, x, h_lora, lora_B, M_words, M_scales, out)
                 if more:
                     for i, s in ((0, a), (1, b)):
                         base_first(s, n, quantised[i])
+                        if (s, n) == (0, 0):
+                            turn_h()
                         if n == BLOCKS - 1:
                             if not by_vector:
                                 for two in range(PASSES // 2):

from contextlib import ExitStack

import concourse.mybir as mybir
from concourse.masks import make_identity

BF16 = mybir.dt.bfloat16
F32 = mybir.dt.float32
I32 = mybir.dt.int32
U32 = mybir.dt.uint32
U8 = mybir.dt.uint8
FP8X4 = mybir.dt.float8_e4m3fn_x4
FP4X4 = mybir.dt.float4_e2m1fn_x4
ADD = mybir.AluOpType.add
MULT = mybir.AluOpType.mult

P = 128
ROWS, IN_F, OUT_F = 1024, 2048, 2048
SEGMENTS = ROWS // P
PAIRS = SEGMENTS // 2
K_PASS = 4 * P
PASSES = IN_F // K_PASS
BANK = 512
BLOCKS = OUT_F // BANK
FIRST_EDGES = (0, K_PASS, 2 * K_PASS, IN_F)
EDGES = (0, 2 * K_PASS, IN_F)
LORA_GAIN = 2.0

TAIL_SPLIT = True
VECTOR_PAIRS = (2, 3)
Q = 32

FLOPS = 2 * ROWS * IN_F * OUT_F + 2 * ROWS * P * OUT_F


def tile_lorasequential_pa_kernel(tc, x, h_lora, lora_B, M_words, M_scales, out):
    nc = tc.nc
    with ExitStack() as stack:
        resident = stack.enter_context(tc.tile_pool(name="resident", bufs=1))
        operand = stack.enter_context(tc.tile_pool(name="operand", bufs=4))
        turned_pool = stack.enter_context(tc.psum_pool(name="turned_pool", bufs=3))
        lora_pool = stack.enter_context(tc.psum_pool(name="lora_pool", bufs=2))
        base_pool = stack.enter_context(tc.psum_pool(name="base_pool", bufs=3))
        stack.enter_context(tc.manual_schedule())

        x_sb = [resident.tile([P, IN_F], BF16, name="x_sb%d" % s) for s in range(SEGMENTS) if s // 2 not in VECTOR_PAIRS]
        landed = dict(
            (pair, resident.tile([P, PASSES, 2 * P // Q, P], BF16, name="landed%d" % pair)) for pair in VECTOR_PAIRS
        )
        turning = stack.enter_context(tc.tile_pool(name="turning", bufs=1))
        b_sb = [resident.tile([P, OUT_F], BF16, name="b_sb%d" % s) for s in range(SEGMENTS)]
        out_sb = [resident.tile([P, OUT_F], F32, name="out_sb%d" % s) for s in range(SEGMENTS)]
        h_sb = resident.tile([P, SEGMENTS, P], BF16)
        hT_sb = resident.tile([P, ROWS], BF16)
        m_words = [resident.tile([P, PASSES, 2 * BANK], U8, align_bytes=64, name="m_words%d" % n) for n in range(BLOCKS)]
        m_scales = [resident.tile([P, PASSES, BANK], U8, align_bytes=64, name="m_scales%d" % n) for n in range(BLOCKS)]
        ident_f32 = resident.tile([P, P], F32)
        ident_bf16 = resident.tile([P, P], BF16)

        make_identity(nc, ident_f32[:])
        make_identity(nc, ident_bf16[:])

        idle = resident.tile([P, BANK], BF16)
        nc.vector.memset(idle[:], 0.0)
        warm = resident.tile([P, 1], F32)
        nc.vector.memset(warm[:], 0.0)
        nc.scalar.mul(out=warm[:], in_=warm[:], mul=LORA_GAIN)

        for n in range(BLOCKS):
            nc.vector.memset(m_scales[n][:].rearrange("p g c -> p (g c)").bitcast(I32), 0)

        def load_x(s, edges):
            for first, last in zip(edges[:-1], edges[1:]):
                nc.sync.dma_start(out=x_sb[s][:, first:last], in_=x[P * s : P * (s + 1), first:last])

        def load_x_by_quadrants(pair):
            for g in range(PASSES):
                for c in (0, 2, 1, 3):
                    first = K_PASS * g + P * c
                    nc.sync.dma_start(
                        out=landed[pair][Q * c : Q * (c + 1), g, :, :],
                        in_=x[2 * P * pair : 2 * P * (pair + 1), first : first + P].rearrange("(R q) e -> q R e", q=Q),
                    )

        def load_lora_b(s):
            nc.sync.dma_start(out=b_sb[s][:], in_=lora_B[s])

        def load_h():
            nc.sync.dma_start(
                out=h_sb[:], in_=h_lora.rearrange("s b r -> (s b) r").rearrange("(p j) r -> p j r", j=SEGMENTS)
            )

        def load_m_block(n, pieces):
            cols = slice(BANK * n, BANK * (n + 1))
            for r in range(4):
                nc.sync.dma_start(
                    out=m_scales[n][r:P:32, :, :].bitcast(I32),
                    in_=M_scales[:, r:16:4, cols].rearrange("g q c -> q g c").bitcast(I32),
                )
            byte_cols = slice(2 * BANK * n, 2 * BANK * (n + 1))
            count = PASSES // pieces
            for piece in range(pieces):
                some = slice(count * piece, count * (piece + 1))
                nc.sync.dma_start(
                    out=m_words[n][:, some, :].bitcast(I32),
                    in_=M_words[some, :, byte_cols].rearrange("g p c -> p g c").bitcast(I32),
                )

        load_x(0, FIRST_EDGES)
        load_x(1, EDGES)
        load_m_block(0, 2)
        load_h()
        for n in range(1, BLOCKS):
            load_m_block(n, 1)
        load_x(2, (0, IN_F))
        load_x(3, (0, IN_F))
        load_lora_b(0)
        load_lora_b(1)
        load_x_by_quadrants(2)
        load_lora_b(2)
        load_lora_b(3)
        load_x_by_quadrants(3)
        for s in range(4, SEGMENTS):
            load_lora_b(s)

        def sort_x(s, edges=(0, IN_F)):
            sorted_words = operand.tile([P, IN_F // 2], F32, tag="sorted_words")
            for first, last in zip(edges[:-1], edges[1:]):
                cols = slice(first // 2, last // 2)
                nc.vector.tensor_copy(
                    out=sorted_words[:, cols].rearrange("r (g u p) -> r g u p", u=2, p=P),
                    in_=x_sb[s][:].bitcast(F32)[:, cols].rearrange("r (g p u) -> r g u p", u=2, p=P),
                )
            return sorted_words

        def turn_two_passes(words, is_sorted, two, grouped, by_vector=False):
            turned = turned_pool.tile([P, 4, P], F32, tag="turned")
            for j in range(4):
                if is_sorted:
                    source = words[:, P * (4 * two + j) : P * (4 * two + j + 1)]
                else:
                    g, u = 2 * two + j // 2, j % 2
                    source = words[:, 2 * P * g + u : 2 * P * (g + 1) : 2]
                nc.tensor.transpose(turned[:, j, :], source, ident_f32[:])
            grouped_words = grouped[:].bitcast(F32).rearrange("p (g r u) -> p g r u", r=P, u=2)
            if by_vector:
                nc.vector.tensor_copy(
                    out=grouped_words[:, 2 * two : 2 * two + 2, :, :],
                    in_=turned[:].rearrange("p (g u) r -> p g r u", u=2),
                )
            else:
                nc.scalar.copy(
                    out=grouped_words[:, 2 * two : 2 * two + 2, :, :],
                    in_=turned[:].rearrange("p (g u) r -> p g r u", u=2),
                )

        def turn_by_vector(pair, two, parted, turned_words):
            half = IN_F // 2
            cols = slice(half * two, half * (two + 1))
            nc.vector.tensor_copy(
                out=parted[:, cols].rearrange("r (j u c) -> r j u c", u=2, c=Q),
                in_=landed[pair][:, 2 * two : 2 * two + 2, :, :]
                .rearrange("r g R e -> r (g R e)")
                .bitcast(F32)
                .rearrange("r (j c u) -> r j u c", u=2, c=Q),
            )
            nc.vector.transpose(out=turned_words[:, cols], in_=parted[:, cols])

        def group_words(turned_words, i, g, grouped):
            nc.scalar.copy(
                out=grouped[:].bitcast(F32).rearrange("p (g R q u) -> p g R q u", g=PASSES, q=Q, u=2)[:, g, :, :, :],
                in_=turned_words[:].rearrange("p (g R u q) -> p g R q u", g=PASSES, u=2, q=Q)[
                    :, g, P // Q * i : P // Q * (i + 1), :, :
                ],
            )

        def new_grouped():
            grouped = operand.tile([P, IN_F], BF16, align_bytes=64, tag="grouped")
            return grouped

        def new_quantised():
            codes = operand.tile([P, PASSES * P], U32, align_bytes=64, tag="codes")
            scales = operand.tile([P, PASSES * P], U8, align_bytes=64, tag="scales")
            return codes, scales

        def quantise(grouped, quantised, first_pass, passes):
            codes, scales = quantised
            cols = slice(P * first_pass, P * (first_pass + passes))
            nc.vector.quantize_mx(
                out=codes[:, cols].bitcast(FP8X4),
                scales=scales[:, cols],
                in_=grouped[:, 4 * P * first_pass : 4 * P * (first_pass + passes)],
            )

        def turn_h():
            hT_ps = turned_pool.tile([P, SEGMENTS, P], BF16, tag="turned")
            for j in range(SEGMENTS):
                nc.tensor.transpose(hT_ps[:, j, :], h_sb[:, j, :], ident_bf16[:])
            nc.vector.tensor_copy(
                out=hT_sb[:].rearrange("r (p j) -> r p j", j=SEGMENTS), in_=hT_ps[:].rearrange("r j p -> r p j")
            )

        def lora_product(s, n, in_turned_bank=False):
            if in_turned_bank:
                low_rank = turned_pool.tile([P, BANK], F32, tag="turned")
            else:
                low_rank = lora_pool.tile([P, BANK], F32, tag="low_rank")
            nc.tensor.matmul(
                out=low_rank[:],
                lhsT=hT_sb[:, P * s : P * (s + 1)],
                rhs=b_sb[s][:, BANK * n : BANK * (n + 1)],
                start=True,
                stop=True,
            )
            return low_rank

        def lora_first(s, n, in_turned_bank=False):
            nc.scalar.mul(
                out=out_sb[s][:, BANK * n : BANK * (n + 1)], in_=lora_product(s, n, in_turned_bank)[:], mul=LORA_GAIN
            )

        def group(n, quantised, first_col, width, in_turned_bank=False):
            codes, scales = quantised
            if in_turned_bank:
                base_sum = turned_pool.tile([P, BANK], F32, tag="turned")
            else:
                base_sum = base_pool.tile([P, BANK], F32, tag="base_sum")
            for g in range(PASSES):
                rows = slice(P * g, P * (g + 1))
                nc.tensor.matmul_mx(
                    out=base_sum[:, 0:width],
                    lhsT=codes[:, rows].bitcast(FP8X4),
                    lhsT_scale=scales[:, rows],
                    rhs=m_words[n][:, g, 2 * first_col : 2 * (first_col + width)].bitcast(FP4X4),
                    rhs_scale=m_scales[n][:, g, first_col : first_col + width],
                    start=(g == 0),
                    stop=(g == PASSES - 1),
                )
            return base_sum

        def store(s, cols):
            nc.sync.dma_start(out=out[P * s : P * (s + 1), cols], in_=out_sb[s][:, cols])

        def store_two_blocks(s, n):
            if s >= SEGMENTS - 4 and n >= 2:
                store(s, slice(BANK * n, BANK * (n + 1)))
            elif n % 2 == 1:
                store(s, slice(BANK * (n - 1), BANK * (n + 1)))

        def add_and_store(s, n, base_sum, first_col, width):
            cols = slice(BANK * n + first_col, BANK * n + first_col + width)
            nc.vector.tensor_tensor(out=out_sb[s][:, cols], in0=base_sum[:, 0:width], in1=out_sb[s][:, cols], op=ADD)
            store(s, cols)

        def base_first(s, n, quantised):
            nc.scalar.copy(out=out_sb[s][:, BANK * n : BANK * (n + 1)], in_=group(n, quantised, 0, BANK)[:])

        def lora_second(s, n, in_turned_bank):
            cols = slice(BANK * n, BANK * (n + 1))
            nc.vector.scalar_tensor_tensor(
                out=out_sb[s][:, cols],
                in0=lora_product(s, n, in_turned_bank)[:],
                scalar=LORA_GAIN,
                in1=out_sb[s][:, cols],
                op0=MULT,
                op1=ADD,
            )
            store_two_blocks(s, n)

        def block(s, n, quantised, in_turned_bank=False):
            add_and_store(s, n, group(n, quantised, 0, BANK, in_turned_bank), 0, BANK)

        def idle_products(count):
            for n in range(count):
                unread = lora_pool.tile([P, BANK], F32, tag="low_rank")
                nc.tensor.matmul(out=unread[:], lhsT=idle[:, 0:P], rhs=idle[:], start=True, stop=True)

        idle_products(4)
        quantised = []
        sorted_first = [sort_x(0, FIRST_EDGES), sort_x(1, EDGES)]
        for s in (0, 1):
            grouped = new_grouped()
            fresh = new_quantised()
            for two in range(PASSES // 2):
                turn_two_passes(sorted_first[s][:], True, two, grouped)
                quantise(grouped, fresh, 2 * two, 2)
            quantised.append(fresh)

        for pair in range(PAIRS):
            a, b = 2 * pair, 2 * pair + 1
            more = pair + 1 < PAIRS
            by_vector = pair + 1 in VECTOR_PAIRS
            for n in range(BLOCKS):
                if pair > 0 and (n % 2 == 0 or not more):
                    for j in (n, n + 1) if more else (n,):
                        lora_second(a - 2, j, False)
                        lora_second(b - 2, j, True)
                if not more:
                    lora_first(a, n, True)
                    lora_first(b, n, True)
                if n == BLOCKS - 1 and more:
                    quantised_next = [new_quantised(), new_quantised()]
                if n == BLOCKS - 1 and more and not by_vector:
                    grouped_next = [new_grouped(), new_grouped()]
                if more:
                    for i, s in ((0, a), (1, b)):
                        base_first(s, n, quantised[i])
                        if (s, n) == (0, 0):
                            turn_h()
                        if n == BLOCKS - 1:
                            if not by_vector:
                                for two in range(PASSES // 2):
                                    turn_two_passes(sorted_next[i][:], True, two, grouped_next[i], two == 1)
                            quantise(grouped_next[i], quantised_next[i], 0, PASSES)
                else:
                    block(a, n, quantised[0])
                    if n < BLOCKS - 1 or not TAIL_SPLIT:
                        block(b, n, quantised[1])
                    else:
                        for first_col in range(0, BANK, P):
                            add_and_store(b, n, group(n, quantised[1], first_col, P, first_col % (2 * P) == P), first_col, P)
                if n == 0 and more and not by_vector:
                    sorted_next = [sort_x(a + 2), sort_x(b + 2)]
                if n in (1, 2) and by_vector:
                    if n == 1:
                        parted = turning.tile([P, IN_F], F32, align_bytes=64, tag="parted")
                        turned_words = turning.tile([P, IN_F], F32, align_bytes=64, tag="turned_words")
                        grouped_next = [new_grouped(), new_grouped()]
                        for two in range(PASSES // 2):
                            turn_by_vector(pair + 1, two, parted, turned_words)
                    for i in (0, 1):
                        for g in (2 * n - 2, 2 * n - 1):
                            group_words(turned_words, i, g, grouped_next[i])
            if more:
                quantised = quantised_next
